import numpy as np
import ml_dtypes


def mxq(x, axis, fmt="e4m3"):
    dtype, down = {"e4m3": (ml_dtypes.float8_e4m3fn, 7), "e5m2": (ml_dtypes.float8_e5m2, 14)}[fmt]
    v = np.moveaxis(np.asarray(x, np.float32).astype(ml_dtypes.bfloat16).astype(np.float64), axis, -1)
    blocks = v.reshape(v.shape[:-1] + (-1, 32))
    amax = np.abs(blocks).max(-1, keepdims=True)
    byte = np.maximum(np.where(amax > 0, np.frexp(amax)[1] - 1 + 127, 0) - down, 1)
    scale = np.exp2(byte - 127.0)
    codes = (blocks / scale).astype(np.float32).astype(dtype).astype(np.float64)
    return np.moveaxis((codes * scale).reshape(v.shape), -1, axis)


WIDE = False


def mx_kscale(k):
    if not WIDE:
        return np.ones(k)
    levels = np.array([10, -10, 5, -5, 0])
    a = np.random.permutation(np.resize(levels, k // 512 * 4)).reshape(k // 512, 4)
    idx = np.arange(k)
    return np.exp2(a[idx // 512, idx % 128 // 32])


BF16 = ml_dtypes.bfloat16


def bf(x):
    return np.asarray(x, np.float32).astype(BF16)


def f64(x):
    return np.asarray(x).astype(np.float64)


B, D, H = 256, 512, 2048
C = D + H
EPS = 1e-3


def sigmoid(v):
    return 1.0 / (1.0 + np.exp(-v))


def layer_norm(v, gamma, beta):
    m = v.mean(-1, keepdims=True)
    var = v.var(-1, keepdims=True)
    return (v - m) / np.sqrt(var + EPS) * gamma + beta


def setup_inputs():
    s = mx_kscale(D)
    t = mx_kscale(H)
    w_u = np.random.standard_normal((C, H)) / np.sqrt(C)
    w_u[:D] = w_u[:D] / s[:, None]
    g = np.random.standard_normal((B, H))
    return {"x": bf(np.random.standard_normal((B, D)) * s),
            "hidden_state": bf(np.random.standard_normal((B, H))),
            "swiglu": bf(g / (1.0 + np.exp(-g)) * np.random.standard_normal((B, H))),
            "W_u": bf(w_u),
            "b_u": bf(np.random.standard_normal(H) * 0.3),
            "gamma_h": bf((1.0 + 0.1 * np.random.standard_normal(H)) * t),
            "beta_h": bf(0.1 * np.random.standard_normal(H) * t),
            "W_d": bf(np.random.standard_normal((H, D)) / np.sqrt(H) / t[:, None]),
            "b_d": bf(np.random.standard_normal(D) * 0.3),
            "gamma_o": bf(1.0 + 0.1 * np.random.standard_normal(D)),
            "beta_o": bf(0.1 * np.random.standard_normal(D))}


def reference(x, hidden_state, swiglu, W_u, b_u, gamma_h, beta_h, W_d, b_d, gamma_o, beta_o):
    h = f64(hidden_state)
    combined = np.concatenate([f64(x), h], axis=-1)
    u = sigmoid((mxq(combined, 1, "e4m3") @ mxq(f64(W_u), 0, "e4m3")) + f64(b_u))
    new_h = layer_norm((1.0 - u) * h + u * f64(swiglu) + h, f64(gamma_h), f64(beta_h))
    out = layer_norm((mxq(new_h, 1, "e4m3") @ mxq(f64(W_d), 0, "e4m3")) + f64(b_d), f64(gamma_o), f64(beta_o))
    return out, new_h

@@ -1,0 +1,275 @@
+from contextlib import ExitStack
+
+import concourse.mybir as mybir
+from concourse.masks import make_identity
+
+F32 = mybir.dt.float32
+BF16 = mybir.dt.bfloat16
+U32 = mybir.dt.uint32
+U8 = mybir.dt.uint8
+FP8X4 = mybir.dt.float8_e4m3fn_x4
+ALU = mybir.AluOpType
+ACT = mybir.ActivationFunctionType
+
+P = 128
+PACK = 4
+K_PASS = P * PACK
+BANK = 512
+
+B, D, H = 256, 512, 2048
+C = D + H
+EPS = 1e-3
+B_TILES = B // P
+U_PASSES = C // K_PASS
+D_PASSES = H // K_PASS
+BLOCKS = H // BANK
+H_TILES = BANK // P
+
+VECTOR_COLS = 192
+RUN = 4
+
+GAMMA_H_AT, BETA_H_AT, B_D_AT, GAMMA_O_AT, BETA_O_AT = 0, H, 2 * H, 2 * H + D, 2 * H + 2 * D
+VEC_COLS = 2 * H + 3 * D
+
+FLOPS = 2 * B * C * H + 2 * B * H * D
+
+
+def tile_recurrentffn_pb_kernel(
+    tc, x, hidden_state, swiglu, W_u, b_u, gamma_h, beta_h, W_d, b_d, gamma_o, beta_o, out_0, out_1
+):
+    nc = tc.nc
+    with ExitStack() as ctx:
+        const = ctx.enter_context(tc.tile_pool(name="const", bufs=1))
+        raw_pool = ctx.enter_context(tc.tile_pool(name="raw", bufs=12))
+        grouped_pool = ctx.enter_context(tc.tile_pool(name="grouped", bufs=4))
+        wu_pool = ctx.enter_context(tc.tile_pool(name="wu", bufs=2 * U_PASSES))
+        work = ctx.enter_context(tc.tile_pool(name="work", bufs=2))
+        psum_acc = ctx.enter_context(tc.psum_pool(name="psum_acc", bufs=3))
+        psum_turn = ctx.enter_context(tc.psum_pool(name="psum_turn", bufs=3))
+        psum_spread = ctx.enter_context(tc.psum_pool(name="psum_spread", bufs=2))
+
+        def load_chunk(view):
+            raw = raw_pool.tile([P, PACK, BANK], BF16, name="raw", tag="raw")
+            nc.sync.dma_start(out=raw[:], in_=view)
+            return raw
+
+        def load_block(block):
+            cols = slice(block * BANK, (block + 1) * BANK)
+            wu_raw = [
+                load_chunk(W_u[g * K_PASS : (g + 1) * K_PASS, cols].rearrange("(q j) w -> q j w", j=PACK))
+                for g in range(U_PASSES)
+            ]
+            wd_raw = load_chunk(W_d[block * K_PASS : (block + 1) * K_PASS, :].rearrange("(j q) w -> q j w", q=P))
+            return wu_raw, wd_raw
+
+        def quantise_chunk(raw, codes, scales):
+            grouped = grouped_pool.tile([P, BANK, PACK], BF16, name="grouped", tag="grouped", align_bytes=64)
+            src = raw[:].rearrange("q j (c i) -> q c j i", i=RUN)
+            dst = grouped[:].rearrange("q (c i) j -> q c j i", i=RUN)
+            split = VECTOR_COLS // RUN
+            nc.vector.tensor_copy(out=dst[:, :split], in_=src[:, :split])
+            nc.scalar.copy(out=dst[:, split:], in_=src[:, split:])
+            nc.vector.quantize_mx(
+                out=codes.bitcast(FP8X4), scales=scales, in_=grouped[:].rearrange("q w j -> q (w j)")
+            )
+
+        ident = const.tile([P, P], F32, name="ident")
+        make_identity(nc, ident[:])
+        ones = const.tile([P, P], BF16, name="ones")
+        nc.vector.memset(ones[:], 1.0)
+        neg_half = const.tile([P, B_TILES], F32, name="neg_half")
+        nc.vector.memset(neg_half[:], -0.5)
+
+        vec_rows = const.tile([P, VEC_COLS], BF16, name="vec_rows")
+        nc.vector.memset(vec_rows[:], 0.0)
+        for vec, at in (
+            (gamma_h, GAMMA_H_AT), (beta_h, BETA_H_AT), (b_d, B_D_AT), (gamma_o, GAMMA_O_AT), (beta_o, BETA_O_AT)
+        ):
+            nc.scalar.dma_start(
+                out=vec_rows[0:1, at : at + vec.shape[0]], in_=vec.rearrange("(o n) -> o n", o=1)
+            )
+
+        def spread(at):
+            bank = psum_spread.tile([P, BANK], F32, name="spread_bank", tag="spread")
+            nc.tensor.matmul(out=bank[:], lhsT=ones[:], rhs=vec_rows[:, at : at + BANK], start=True, stop=True)
+            return bank
+
+        bu_loaded = const.tile([H // P, P], BF16, name="bu_loaded")
+        nc.scalar.dma_start(out=bu_loaded[:], in_=b_u.rearrange("(c q) -> c q", q=P))
+        bu_rows = const.tile([P, P], F32, name="bu_rows")
+        nc.vector.memset(bu_rows[:], 0.0)
+        nc.vector.tensor_copy(out=bu_rows[0 : H // P, :], in_=bu_loaded[:])
+
+        next_block = load_block(0)
+        x_sb = const.tile([P, B_TILES, D], BF16, name="x_sb")
+        nc.sync.dma_start(out=x_sb[:], in_=x.rearrange("(t r) k -> r t k", r=P))
+        h_sb = const.tile([P, B_TILES, H], BF16, name="h_sb")
+        nc.sync.dma_start(out=h_sb[:], in_=hidden_state.rearrange("(t r) k -> r t k", r=P))
+        s_sb = const.tile([P, B_TILES, H], BF16, name="s_sb")
+        nc.sync.dma_start(out=s_sb[:], in_=swiglu.rearrange("(t r) k -> r t k", r=P))
+
+        bu_turned = psum_turn.tile([P, P], F32, name="bu_turned", tag="turn")
+        nc.tensor.transpose(bu_turned[:], bu_rows[:], ident[:])
+        bias_u = const.tile([P, H // P], F32, name="bias_u")
+        nc.vector.tensor_copy(out=bias_u[:], in_=bu_turned[:, 0 : H // P])
+
+        bd_bank = spread(B_D_AT)
+        bd_all = const.tile([P, D], F32, name="bd_all")
+        nc.scalar.copy(out=bd_all[:], in_=bd_bank[:])
+
+        comb_codes = const.tile([P, U_PASSES, B], U32, name="comb_codes", align_bytes=64)
+        comb_scales = const.tile([P, U_PASSES, B], U8, name="comb_scales", align_bytes=64)
+        for g in range(U_PASSES):
+            turned = psum_turn.tile([P, 2, B], F32, name="turned", tag="turn")
+            for t in range(B_TILES):
+                feats = x_sb[:, t, :] if g == 0 else h_sb[:, t, (g - 1) * K_PASS : g * K_PASS]
+                words = feats.bitcast(F32).rearrange("r (q u) -> r u q", u=2)
+                for u in range(2):
+                    nc.tensor.transpose(turned[:, u, t * P : (t + 1) * P], words[:, u, :], ident[:])
+            act_grouped = work.tile([P, B, PACK], BF16, name="act_grouped", tag="act_grouped", align_bytes=64)
+            nc.scalar.copy(
+                out=act_grouped[:].rearrange("q r j -> q (r j)").bitcast(F32).rearrange("q (r u) -> q r u", u=2),
+                in_=turned[:].rearrange("q u r -> q r u"),
+            )
+            nc.vector.quantize_mx(
+                out=comb_codes[:, g, :].bitcast(FP8X4),
+                scales=comb_scales[:, g, :],
+                in_=act_grouped[:].rearrange("q r j -> q (r j)"),
+            )
+
+        wd_codes = const.tile([P, D_PASSES, D], U32, name="wd_codes", align_bytes=64)
+        wd_scales = const.tile([P, D_PASSES, D], U8, name="wd_scales", align_bytes=64)
+        blend = const.tile([P, B_TILES, H], F32, name="blend")
+        blend_sums = const.tile([P, B_TILES, BLOCKS], F32, name="blend_sums")
+        for block in range(BLOCKS):
+            wu_raw, wd_raw = next_block
+            if block + 1 < BLOCKS:
+                next_block = load_block(block + 1)
+            wu_codes, wu_scales = [], []
+            for g in range(U_PASSES):
+                wu_codes.append(wu_pool.tile([P, BANK], U32, name="wu_codes", tag="wu_codes", align_bytes=64))
+                wu_scales.append(wu_pool.tile([P, BANK], U8, name="wu_scales", tag="wu_scales", align_bytes=64))
+                quantise_chunk(wu_raw[g], wu_codes[g][:], wu_scales[g][:])
+            quantise_chunk(wd_raw, wd_codes[:, block, :], wd_scales[:, block, :])
+
+            u_turned = []
+            for c in range(H_TILES):
+                m_cols = slice(c * P, (c + 1) * P)
+                acc = psum_acc.tile([P, B], F32, name="acc", tag="acc")
+                for g in range(U_PASSES):
+                    nc.tensor.matmul_mx(
+                        out=acc[:],
+                        lhsT=wu_codes[g][:, m_cols].bitcast(FP8X4),
+                        lhsT_scale=wu_scales[g][:, m_cols],
+                        rhs=comb_codes[:, g, :].bitcast(FP8X4),
+                        rhs_scale=comb_scales[:, g, :],
+                        start=(g == 0),
+                        stop=(g == U_PASSES - 1),
+                    )
+                u_turned.append(work.tile([P, B], F32, name="u_turned", tag="u_turned", bufs=2 * H_TILES))
+                feature_tile = block * H_TILES + c
+                nc.scalar.activation(
+                    out=u_turned[c][:], in_=acc[:], func=ACT.Sigmoid,
+                    bias=bias_u[:, feature_tile : feature_tile + 1], scale=1.0,
+                )
+
+            cols = slice(block * BANK, (block + 1) * BANK)
+            u_bank = [psum_turn.tile([P, BANK], F32, name="u_bank%d" % t, tag="turn") for t in range(B_TILES)]
+            for c in range(H_TILES):
+                for t in range(B_TILES):
+                    nc.tensor.transpose(u_bank[t][:, c * P : (c + 1) * P], u_turned[c][:, t * P : (t + 1) * P], ident[:])
+            diff = [work.tile([P, BANK], F32, name="diff%d" % t, tag="diff", bufs=4) for t in range(B_TILES)]
+            for t in range(B_TILES):
+                nc.vector.tensor_tensor(out=diff[t][:], in0=s_sb[:, t, cols], in1=h_sb[:, t, cols], op=ALU.subtract)
+            for t in range(B_TILES):
+                nc.vector.tensor_tensor(out=diff[t][:], in0=u_bank[t][:], in1=diff[t][:], op=ALU.mult)
+            for t in range(B_TILES):
+                nc.vector.scalar_tensor_tensor(
+                    out=blend[:, t, cols], in0=h_sb[:, t, cols], scalar=2.0, in1=diff[t][:],
+                    op0=ALU.mult, op1=ALU.add, accum_out=blend_sums[:, t, block : block + 1],
+                )
+
+        def layer_norm(values, sums, width, gain_at, shift_at, result, after_piece):
+            neg_mean = work.tile([P, B_TILES], F32, name="neg_mean", tag="neg_mean")
+            nc.vector.tensor_scalar_mul(out=neg_mean[:], in0=sums, scalar1=-1.0 / width)
+            sq_sums = work.tile([P, B_TILES], F32, name="sq_sums", tag="sq_sums")
+            for t in range(B_TILES):
+                squares = work.tile([P, width], BF16, name="squares", tag="squares")
+                nc.scalar.activation(
+                    out=squares[:], in_=values[:, t, :], func=ACT.Square,
+                    bias=neg_mean[:, t : t + 1], scale=1.0, accum_out=sq_sums[:, t : t + 1],
+                )
+            var_eps = work.tile([P, B_TILES], F32, name="var_eps", tag="var_eps")
+            nc.gpsimd.tensor_scalar(
+                out=var_eps[:], in0=sq_sums[:], scalar1=1.0 / width, scalar2=EPS, op0=ALU.mult, op1=ALU.add
+            )
+            rstd = work.tile([P, B_TILES], F32, name="rstd", tag="rstd")
+            nc.gpsimd.tensor_tensor(out=rstd[:], in0=var_eps[:], in1=neg_half[:], op=ALU.pow)
+
+            for i in range(width // BANK):
+                cols = slice(i * BANK, (i + 1) * BANK)
+                gain = spread(gain_at + i * BANK)
+                for t in range(B_TILES):
+                    nc.vector.scalar_tensor_tensor(
+                        out=result[:, t, cols], in0=values[:, t, cols], scalar=neg_mean[:, t : t + 1], in1=gain[:],
+                        op0=ALU.add, op1=ALU.mult,
+                    )
+            for i in range(width // BANK):
+                cols = slice(i * BANK, (i + 1) * BANK)
+                shift = spread(shift_at + i * BANK)
+                for t in range(B_TILES):
+                    nc.vector.scalar_tensor_tensor(
+                        out=result[:, t, cols], in0=result[:, t, cols], scalar=rstd[:, t : t + 1], in1=shift[:],
+                        op0=ALU.mult, op1=ALU.add,
+                    )
+                after_piece(i)
+
+        new_h = const.tile([P, B_TILES, H], F32, name="new_h")
+        nh_codes = const.tile([P, D_PASSES, B], U32, name="nh_codes", align_bytes=64)
+        nh_scales = const.tile([P, D_PASSES, B], U8, name="nh_scales", align_bytes=64)
+        out_acc = [psum_acc.tile([P, D], F32, name="out_acc%d" % t, tag="acc") for t in range(B_TILES)]
+
+        def second_matmul_pass(g):
+            cols = slice(g * K_PASS, (g + 1) * K_PASS)
+            nc.sync.dma_start(out=out_1.rearrange("(t r) k -> r t k", r=P)[:, :, cols], in_=new_h[:, :, cols])
+            act_grouped = work.tile([P, B, PACK], BF16, name="act_grouped", tag="act_grouped", align_bytes=64)
+            for t in range(B_TILES):
+                turned = psum_turn.tile([P, PACK, P], F32, name="turned", tag="turn")
+                for j in range(PACK):
+                    k0 = g * K_PASS + j * P
+                    nc.tensor.transpose(turned[:, j, :], new_h[:, t, k0 : k0 + P], ident[:])
+                nc.scalar.copy(out=act_grouped[:, t * P : (t + 1) * P, :], in_=turned[:].rearrange("q j r -> q r j"))
+            nc.vector.quantize_mx(
+                out=nh_codes[:, g, :].bitcast(FP8X4),
+                scales=nh_scales[:, g, :],
+                in_=act_grouped[:].rearrange("q r j -> q (r j)"),
+            )
+            for t in range(B_TILES):
+                rows = slice(t * P, (t + 1) * P)
+                nc.tensor.matmul_mx(
+                    out=out_acc[t][:],
+                    lhsT=nh_codes[:, g, rows].bitcast(FP8X4),
+                    lhsT_scale=nh_scales[:, g, rows],
+                    rhs=wd_codes[:, g, :].bitcast(FP8X4),
+                    rhs_scale=wd_scales[:, g, :],
+                    start=(g == 0),
+                    stop=(g == D_PASSES - 1),
+                )
+
+        blend_sum = work.tile([P, B_TILES], F32, name="blend_sum", tag="blend_sum")
+        nc.vector.tensor_reduce(out=blend_sum[:], in_=blend_sums[:], axis=mybir.AxisListType.X, op=ALU.add)
+        layer_norm(blend, blend_sum[:], H, GAMMA_H_AT, BETA_H_AT, new_h, second_matmul_pass)
+
+        pre_out = const.tile([P, B_TILES, D], F32, name="pre_out")
+        pre_out_sum = work.tile([P, B_TILES], F32, name="pre_out_sum", tag="pre_out_sum")
+        for t in range(B_TILES):
+            nc.vector.scalar_tensor_tensor(
+                out=pre_out[:, t, :], in0=out_acc[t][:], scalar=1.0, in1=bd_all[:],
+                op0=ALU.mult, op1=ALU.add, accum_out=pre_out_sum[:, t : t + 1],
+            )
+        out_sb = const.tile([P, B_TILES, D], F32, name="out_sb")
+
+        def store_out(piece):
+            nc.sync.dma_start(out=out_0.rearrange("(t r) n -> r t n", r=P), in_=out_sb[:])
+
+        layer_norm(pre_out, pre_out_sum[:], D, GAMMA_O_AT, BETA_O_AT, out_sb, store_out)

@@ -24,6 +24,8 @@ U_PASSES = C // K_PASS
 D_PASSES = H // K_PASS
 BLOCKS = H // BANK
 H_TILES = BANK // P
+WU_CHUNKS = BLOCKS * U_PASSES
+CHUNKS = WU_CHUNKS + D_PASSES
 
 VECTOR_COLS = 192
 RUN = 4
@@ -40,38 +42,12 @@ def tile_recurrentffn_pb_kernel(
     nc = tc.nc
     with ExitStack() as ctx:
         const = ctx.enter_context(tc.tile_pool(name="const", bufs=1))
-        raw_pool = ctx.enter_context(tc.tile_pool(name="raw", bufs=12))
+        raw_pool = ctx.enter_context(tc.tile_pool(name="raw", bufs=8))
         grouped_pool = ctx.enter_context(tc.tile_pool(name="grouped", bufs=4))
-        wu_pool = ctx.enter_context(tc.tile_pool(name="wu", bufs=2 * U_PASSES))
         work = ctx.enter_context(tc.tile_pool(name="work", bufs=2))
         psum_acc = ctx.enter_context(tc.psum_pool(name="psum_acc", bufs=3))
         psum_turn = ctx.enter_context(tc.psum_pool(name="psum_turn", bufs=3))
         psum_spread = ctx.enter_context(tc.psum_pool(name="psum_spread", bufs=2))
-
-        def load_chunk(view):
-            raw = raw_pool.tile([P, PACK, BANK], BF16, name="raw", tag="raw")
-            nc.sync.dma_start(out=raw[:], in_=view)
-            return raw
-
-        def load_block(block):
-            cols = slice(block * BANK, (block + 1) * BANK)
-            wu_raw = [
-                load_chunk(W_u[g * K_PASS : (g + 1) * K_PASS, cols].rearrange("(q j) w -> q j w", j=PACK))
-                for g in range(U_PASSES)
-            ]
-            wd_raw = load_chunk(W_d[block * K_PASS : (block + 1) * K_PASS, :].rearrange("(j q) w -> q j w", q=P))
-            return wu_raw, wd_raw
-
-        def quantise_chunk(raw, codes, scales):
-            grouped = grouped_pool.tile([P, BANK, PACK], BF16, name="grouped", tag="grouped", align_bytes=64)
-            src = raw[:].rearrange("q j (c i) -> q c j i", i=RUN)
-            dst = grouped[:].rearrange("q (c i) j -> q c j i", i=RUN)
-            split = VECTOR_COLS // RUN
-            nc.vector.tensor_copy(out=dst[:, :split], in_=src[:, :split])
-            nc.scalar.copy(out=dst[:, split:], in_=src[:, split:])
-            nc.vector.quantize_mx(
-                out=codes.bitcast(FP8X4), scales=scales, in_=grouped[:].rearrange("q w j -> q (w j)")
-            )
 
         ident = const.tile([P, P], F32, name="ident")
         make_identity(nc, ident[:])
@@ -80,109 +56,142 @@ def tile_recurrentffn_pb_kernel(
         neg_half = const.tile([P, B_TILES], F32, name="neg_half")
         nc.vector.memset(neg_half[:], -0.5)
 
+        bu_loaded = const.tile([H // P, P], BF16, name="bu_loaded")
+        nc.scalar.dma_start(out=bu_loaded[:], in_=b_u.rearrange("(c q) -> c q", q=P))
+        bu_rows = const.tile([P, P], F32, name="bu_rows")
+        nc.vector.memset(bu_rows[:], 0.0)
+        bias_u = const.tile([P, H // P], F32, name="bias_u")
+
         vec_rows = const.tile([P, VEC_COLS], BF16, name="vec_rows")
         nc.vector.memset(vec_rows[:], 0.0)
         for vec, at in (
-            (gamma_h, GAMMA_H_AT), (beta_h, BETA_H_AT), (b_d, B_D_AT), (gamma_o, GAMMA_O_AT), (beta_o, BETA_O_AT)
+            (b_d, B_D_AT), (gamma_h, GAMMA_H_AT), (beta_h, BETA_H_AT), (gamma_o, GAMMA_O_AT), (beta_o, BETA_O_AT)
         ):
             nc.scalar.dma_start(
                 out=vec_rows[0:1, at : at + vec.shape[0]], in_=vec.rearrange("(o n) -> o n", o=1)
             )
+        bd_all = const.tile([P, D], F32, name="bd_all")
 
         def spread(at):
             bank = psum_spread.tile([P, BANK], F32, name="spread_bank", tag="spread")
             nc.tensor.matmul(out=bank[:], lhsT=ones[:], rhs=vec_rows[:, at : at + BANK], start=True, stop=True)
             return bank
 
-        bu_loaded = const.tile([H // P, P], BF16, name="bu_loaded")
-        nc.scalar.dma_start(out=bu_loaded[:], in_=b_u.rearrange("(c q) -> c q", q=P))
-        bu_rows = const.tile([P, P], F32, name="bu_rows")
-        nc.vector.memset(bu_rows[:], 0.0)
-        nc.vector.tensor_copy(out=bu_rows[0 : H // P, :], in_=bu_loaded[:])
+        def turn_small_vectors():
+            nc.vector.tensor_copy(out=bu_rows[0 : H // P, :], in_=bu_loaded[:])
+            bu_turned = psum_turn.tile([P, P], F32, name="bu_turned", tag="turn")
+            nc.tensor.transpose(bu_turned[:], bu_rows[:], ident[:])
+            return bu_turned, spread(B_D_AT)
 
-        next_block = load_block(0)
-        x_sb = const.tile([P, B_TILES, D], BF16, name="x_sb")
-        nc.sync.dma_start(out=x_sb[:], in_=x.rearrange("(t r) k -> r t k", r=P))
-        h_sb = const.tile([P, B_TILES, H], BF16, name="h_sb")
-        nc.sync.dma_start(out=h_sb[:], in_=hidden_state.rearrange("(t r) k -> r t k", r=P))
-        s_sb = const.tile([P, B_TILES, H], BF16, name="s_sb")
-        nc.sync.dma_start(out=s_sb[:], in_=swiglu.rearrange("(t r) k -> r t k", r=P))
+        def keep_small_vectors(bu_turned, bd_bank):
+            nc.vector.tensor_copy(out=bias_u[:], in_=bu_turned[:, 0 : H // P])
+            nc.scalar.copy(out=bd_all[:], in_=bd_bank[:])
 
-        bu_turned = psum_turn.tile([P, P], F32, name="bu_turned", tag="turn")
-        nc.tensor.transpose(bu_turned[:], bu_rows[:], ident[:])
-        bias_u = const.tile([P, H // P], F32, name="bias_u")
-        nc.vector.tensor_copy(out=bias_u[:], in_=bu_turned[:, 0 : H // P])
-
-        bd_bank = spread(B_D_AT)
-        bd_all = const.tile([P, D], F32, name="bd_all")
-        nc.scalar.copy(out=bd_all[:], in_=bd_bank[:])
-
-        comb_codes = const.tile([P, U_PASSES, B], U32, name="comb_codes", align_bytes=64)
-        comb_scales = const.tile([P, U_PASSES, B], U8, name="comb_scales", align_bytes=64)
-        for g in range(U_PASSES):
-            turned = psum_turn.tile([P, 2, B], F32, name="turned", tag="turn")
-            for t in range(B_TILES):
-                feats = x_sb[:, t, :] if g == 0 else h_sb[:, t, (g - 1) * K_PASS : g * K_PASS]
-                words = feats.bitcast(F32).rearrange("r (q u) -> r u q", u=2)
-                for u in range(2):
-                    nc.tensor.transpose(turned[:, u, t * P : (t + 1) * P], words[:, u, :], ident[:])
-            act_grouped = work.tile([P, B, PACK], BF16, name="act_grouped", tag="act_grouped", align_bytes=64)
-            nc.scalar.copy(
-                out=act_grouped[:].rearrange("q r j -> q (r j)").bitcast(F32).rearrange("q (r u) -> q r u", u=2),
-                in_=turned[:].rearrange("q u r -> q r u"),
-            )
-            nc.vector.quantize_mx(
-                out=comb_codes[:, g, :].bitcast(FP8X4),
-                scales=comb_scales[:, g, :],
-                in_=act_grouped[:].rearrange("q r j -> q (r j)"),
-            )
-
+        wu_codes = const.tile([P, WU_CHUNKS, BANK], U32, name="wu_codes", align_bytes=64)
+        wu_scales = const.tile([P, WU_CHUNKS, BANK], U8, name="wu_scales", align_bytes=64)
         wd_codes = const.tile([P, D_PASSES, D], U32, name="wd_codes", align_bytes=64)
         wd_scales = const.tile([P, D_PASSES, D], U8, name="wd_scales", align_bytes=64)
+        raws, groupeds = [], []
+
+        def load_chunk(i):
+            if i < WU_CHUNKS:
+                block, g = divmod(i, U_PASSES)
+                view = W_u[g * K_PASS : (g + 1) * K_PASS, block * BANK : (block + 1) * BANK].rearrange(
+                    "(q j) w -> q j w", j=PACK
+                )
+            else:
+                g = i - WU_CHUNKS
+                view = W_d[g * K_PASS : (g + 1) * K_PASS, :].rearrange("(j q) w -> q j w", q=P)
+            raws.append(raw_pool.tile([P, PACK, BANK], BF16, name="raw", tag="raw"))
+            nc.sync.dma_start(out=raws[i][:], in_=view)
+
+        def regroup_chunk(i):
+            groupeds.append(grouped_pool.tile([P, BANK, PACK], BF16, name="grouped", tag="grouped", align_bytes=64))
+            src = raws[i][:].rearrange("q j (c i) -> q c j i", i=RUN)
+            dst = groupeds[i][:].rearrange("q (c i) j -> q c j i", i=RUN)
+            split = VECTOR_COLS // RUN
+            nc.vector.tensor_copy(out=dst[:, :split], in_=src[:, :split])
+            nc.scalar.copy(out=dst[:, split:], in_=src[:, split:])
+
+        def quantise_chunk(i):
+            if i < WU_CHUNKS:
+                codes, scales = wu_codes[:, i, :], wu_scales[:, i, :]
+            else:
+                codes, scales = wd_codes[:, i - WU_CHUNKS, :], wd_scales[:, i - WU_CHUNKS, :]
+            nc.vector.quantize_mx(
+                out=codes.bitcast(FP8X4), scales=scales, in_=groupeds[i][:].rearrange("q w j -> q (w j)")
+            )
+
+        x_sb = const.tile([P, B_TILES, D], BF16, name="x_sb")
+        h_sb = const.tile([P, B_TILES, H], BF16, name="h_sb")
+        s_sb = const.tile([P, B_TILES, H], BF16, name="s_sb")
+        comb_grouped = const.tile([P, U_PASSES, B, PACK], BF16, name="comb_grouped", align_bytes=64)
+        comb_codes = const.tile([P, U_PASSES, B], U32, name="comb_codes", align_bytes=64)
+        comb_scales = const.tile([P, U_PASSES, B], U8, name="comb_scales", align_bytes=64)
+
+        def turn_activations():
+            for g in range(U_PASSES):
+                turned = psum_turn.tile([P, 2, B], F32, name="turned", tag="turn")
+                for t in range(B_TILES):
+                    feats = x_sb[:, t, :] if g == 0 else h_sb[:, t, (g - 1) * K_PASS : g * K_PASS]
+                    words = feats.bitcast(F32).rearrange("r (q u) -> r u q", u=2)
+                    for u in range(2):
+                        nc.tensor.transpose(turned[:, u, t * P : (t + 1) * P], words[:, u, :], ident[:])
+                nc.scalar.copy(
+                    out=comb_grouped[:, g].rearrange("q r j -> q (r j)").bitcast(F32).rearrange("q (r u) -> q r u", u=2),
+                    in_=turned[:].rearrange("q u r -> q r u"),
+                )
+
+        def quantise_activations():
+            for g in range(U_PASSES):
+                nc.vector.quantize_mx(
+                    out=comb_codes[:, g, :].bitcast(FP8X4),
+                    scales=comb_scales[:, g, :],
+                    in_=comb_grouped[:, g].rearrange("q r j -> q (r j)"),
+                )
+
         blend = const.tile([P, B_TILES, H], F32, name="blend")
         blend_sums = const.tile([P, B_TILES, BLOCKS], F32, name="blend_sums")
-        for block in range(BLOCKS):
-            wu_raw, wd_raw = next_block
-            if block + 1 < BLOCKS:
-                next_block = load_block(block + 1)
-            wu_codes, wu_scales = [], []
-            for g in range(U_PASSES):
-                wu_codes.append(wu_pool.tile([P, BANK], U32, name="wu_codes", tag="wu_codes", align_bytes=64))
-                wu_scales.append(wu_pool.tile([P, BANK], U8, name="wu_scales", tag="wu_scales", align_bytes=64))
-                quantise_chunk(wu_raw[g], wu_codes[g][:], wu_scales[g][:])
-            quantise_chunk(wd_raw, wd_codes[:, block, :], wd_scales[:, block, :])
+        accs, u_banks = [], []
 
-            u_turned = []
+        def first_matmul(block):
             for c in range(H_TILES):
                 m_cols = slice(c * P, (c + 1) * P)
-                acc = psum_acc.tile([P, B], F32, name="acc", tag="acc")
+                accs.append(psum_acc.tile([P, B], F32, name="acc", tag="acc"))
                 for g in range(U_PASSES):
                     nc.tensor.matmul_mx(
-                        out=acc[:],
-                        lhsT=wu_codes[g][:, m_cols].bitcast(FP8X4),
-                        lhsT_scale=wu_scales[g][:, m_cols],
+                        out=accs[block * H_TILES + c][:],
+                        lhsT=wu_codes[:, block * U_PASSES + g, m_cols].bitcast(FP8X4),
+                        lhsT_scale=wu_scales[:, block * U_PASSES + g, m_cols],
                         rhs=comb_codes[:, g, :].bitcast(FP8X4),
                         rhs_scale=comb_scales[:, g, :],
                         start=(g == 0),
                         stop=(g == U_PASSES - 1),
                     )
-                u_turned.append(work.tile([P, B], F32, name="u_turned", tag="u_turned", bufs=2 * H_TILES))
-                feature_tile = block * H_TILES + c
-                nc.scalar.activation(
-                    out=u_turned[c][:], in_=acc[:], func=ACT.Sigmoid,
-                    bias=bias_u[:, feature_tile : feature_tile + 1], scale=1.0,
+
+        def sigmoid_and_turn(block, c):
+            feature_tile = block * H_TILES + c
+            u_turned = work.tile([P, B], F32, name="u_turned", tag="u_turned", bufs=4)
+            nc.scalar.activation(
+                out=u_turned[:], in_=accs[feature_tile][:], func=ACT.Sigmoid,
+                bias=bias_u[:, feature_tile : feature_tile + 1], scale=1.0,
+            )
+            for t in range(B_TILES):
+                if c == 0:
+                    u_banks.append(psum_turn.tile([P, BANK], F32, name="u_bank", tag="turn"))
+                nc.tensor.transpose(
+                    u_banks[block * B_TILES + t][:, c * P : (c + 1) * P], u_turned[:, t * P : (t + 1) * P], ident[:]
                 )
 
+        def blend_block(block):
             cols = slice(block * BANK, (block + 1) * BANK)
-            u_bank = [psum_turn.tile([P, BANK], F32, name="u_bank%d" % t, tag="turn") for t in range(B_TILES)]
-            for c in range(H_TILES):
-                for t in range(B_TILES):
-                    nc.tensor.transpose(u_bank[t][:, c * P : (c + 1) * P], u_turned[c][:, t * P : (t + 1) * P], ident[:])
             diff = [work.tile([P, BANK], F32, name="diff%d" % t, tag="diff", bufs=4) for t in range(B_TILES)]
             for t in range(B_TILES):
                 nc.vector.tensor_tensor(out=diff[t][:], in0=s_sb[:, t, cols], in1=h_sb[:, t, cols], op=ALU.subtract)
             for t in range(B_TILES):
-                nc.vector.tensor_tensor(out=diff[t][:], in0=u_bank[t][:], in1=diff[t][:], op=ALU.mult)
+                nc.vector.tensor_tensor(
+                    out=diff[t][:], in0=u_banks[block * B_TILES + t][:], in1=diff[t][:], op=ALU.mult
+                )
             for t in range(B_TILES):
                 nc.vector.scalar_tensor_tensor(
                     out=blend[:, t, cols], in0=h_sb[:, t, cols], scalar=2.0, in1=diff[t][:],
@@ -190,6 +199,7 @@ def tile_recurrentffn_pb_kernel(
                 )
 
         def layer_norm(values, sums, width, gain_at, shift_at, result, after_piece):
+            pieces = width // BANK
             neg_mean = work.tile([P, B_TILES], F32, name="neg_mean", tag="neg_mean")
             nc.vector.tensor_scalar_mul(out=neg_mean[:], in0=sums, scalar1=-1.0 / width)
             sq_sums = work.tile([P, B_TILES], F32, name="sq_sums", tag="sq_sums")
@@ -206,70 +216,107 @@ def tile_recurrentffn_pb_kernel(
             rstd = work.tile([P, B_TILES], F32, name="rstd", tag="rstd")
             nc.gpsimd.tensor_tensor(out=rstd[:], in0=var_eps[:], in1=neg_half[:], op=ALU.pow)
 
-            for i in range(width // BANK):
+            gain = [spread(gain_at + i * BANK) for i in range(min(2, pieces))]
+            for i in range(pieces):
                 cols = slice(i * BANK, (i + 1) * BANK)
-                gain = spread(gain_at + i * BANK)
                 for t in range(B_TILES):
                     nc.vector.scalar_tensor_tensor(
-                        out=result[:, t, cols], in0=values[:, t, cols], scalar=neg_mean[:, t : t + 1], in1=gain[:],
+                        out=result[:, t, cols], in0=values[:, t, cols], scalar=neg_mean[:, t : t + 1], in1=gain[i][:],
                         op0=ALU.add, op1=ALU.mult,
                     )
-            for i in range(width // BANK):
+                if i + 2 < pieces:
+                    gain.append(spread(gain_at + (i + 2) * BANK))
+            shift = [spread(shift_at + i * BANK) for i in range(min(2, pieces))]
+            for i in range(pieces):
                 cols = slice(i * BANK, (i + 1) * BANK)
-                shift = spread(shift_at + i * BANK)
                 for t in range(B_TILES):
                     nc.vector.scalar_tensor_tensor(
-                        out=result[:, t, cols], in0=result[:, t, cols], scalar=rstd[:, t : t + 1], in1=shift[:],
+                        out=result[:, t, cols], in0=result[:, t, cols], scalar=rstd[:, t : t + 1], in1=shift[i][:],
                         op0=ALU.mult, op1=ALU.add,
                     )
+                if i + 2 < pieces:
+                    shift.append(spread(shift_at + (i + 2) * BANK))
                 after_piece(i)
 
         new_h = const.tile([P, B_TILES, H], F32, name="new_h")
+        nh_grouped = const.tile([P, D_PASSES, B, PACK], BF16, name="nh_grouped", align_bytes=64)
         nh_codes = const.tile([P, D_PASSES, B], U32, name="nh_codes", align_bytes=64)
         nh_scales = const.tile([P, D_PASSES, B], U8, name="nh_scales", align_bytes=64)
-        out_acc = [psum_acc.tile([P, D], F32, name="out_acc%d" % t, tag="acc") for t in range(B_TILES)]
 
-        def second_matmul_pass(g):
+        def store_and_turn_new_h(g):
             cols = slice(g * K_PASS, (g + 1) * K_PASS)
             nc.sync.dma_start(out=out_1.rearrange("(t r) k -> r t k", r=P)[:, :, cols], in_=new_h[:, :, cols])
-            act_grouped = work.tile([P, B, PACK], BF16, name="act_grouped", tag="act_grouped", align_bytes=64)
             for t in range(B_TILES):
                 turned = psum_turn.tile([P, PACK, P], F32, name="turned", tag="turn")
                 for j in range(PACK):
                     k0 = g * K_PASS + j * P
                     nc.tensor.transpose(turned[:, j, :], new_h[:, t, k0 : k0 + P], ident[:])
-                nc.scalar.copy(out=act_grouped[:, t * P : (t + 1) * P, :], in_=turned[:].rearrange("q j r -> q r j"))
-            nc.vector.quantize_mx(
-                out=nh_codes[:, g, :].bitcast(FP8X4),
-                scales=nh_scales[:, g, :],
-                in_=act_grouped[:].rearrange("q r j -> q (r j)"),
-            )
-            for t in range(B_TILES):
-                rows = slice(t * P, (t + 1) * P)
-                nc.tensor.matmul_mx(
-                    out=out_acc[t][:],
-                    lhsT=nh_codes[:, g, rows].bitcast(FP8X4),
-                    lhsT_scale=nh_scales[:, g, rows],
-                    rhs=wd_codes[:, g, :].bitcast(FP8X4),
-                    rhs_scale=wd_scales[:, g, :],
-                    start=(g == 0),
-                    stop=(g == D_PASSES - 1),
-                )
+                nc.scalar.copy(out=nh_grouped[:, g, t * P : (t + 1) * P, :], in_=turned[:].rearrange("q j r -> q r j"))
 
-        blend_sum = work.tile([P, B_TILES], F32, name="blend_sum", tag="blend_sum")
-        nc.vector.tensor_reduce(out=blend_sum[:], in_=blend_sums[:], axis=mybir.AxisListType.X, op=ALU.add)
-        layer_norm(blend, blend_sum[:], H, GAMMA_H_AT, BETA_H_AT, new_h, second_matmul_pass)
+        def second_matmul(out_acc):
+            for g in range(D_PASSES):
+                nc.vector.quantize_mx(
+                    out=nh_codes[:, g, :].bitcast(FP8X4),
+                    scales=nh_scales[:, g, :],
+                    in_=nh_grouped[:, g].rearrange("q r j -> q (r j)"),
+                )
+                for t in range(B_TILES):
+                    rows = slice(t * P, (t + 1) * P)
+                    nc.tensor.matmul_mx(
+                        out=out_acc[t][:],
+                        lhsT=nh_codes[:, g, rows].bitcast(FP8X4),
+                        lhsT_scale=nh_scales[:, g, rows],
+                        rhs=wd_codes[:, g, :].bitcast(FP8X4),
+                        rhs_scale=wd_scales[:, g, :],
+                        start=(g == 0),
+                        stop=(g == D_PASSES - 1),
+                    )
 
         pre_out = const.tile([P, B_TILES, D], F32, name="pre_out")
-        pre_out_sum = work.tile([P, B_TILES], F32, name="pre_out_sum", tag="pre_out_sum")
-        for t in range(B_TILES):
-            nc.vector.scalar_tensor_tensor(
-                out=pre_out[:, t, :], in0=out_acc[t][:], scalar=1.0, in1=bd_all[:],
-                op0=ALU.mult, op1=ALU.add, accum_out=pre_out_sum[:, t : t + 1],
-            )
         out_sb = const.tile([P, B_TILES, D], F32, name="out_sb")
 
         def store_out(piece):
             nc.sync.dma_start(out=out_0.rearrange("(t r) n -> r t n", r=P), in_=out_sb[:])
 
-        layer_norm(pre_out, pre_out_sum[:], D, GAMMA_O_AT, BETA_O_AT, out_sb, store_out)
+        with tc.manual_schedule():
+            for i in range(CHUNKS):
+                load_chunk(i)
+                if i == 1:
+                    nc.sync.dma_start(out=x_sb[:], in_=x.rearrange("(t r) k -> r t k", r=P))
+                    nc.sync.dma_start(out=h_sb[:], in_=hidden_state.rearrange("(t r) k -> r t k", r=P))
+                if i == U_PASSES - 1:
+                    nc.sync.dma_start(out=s_sb[:], in_=swiglu.rearrange("(t r) k -> r t k", r=P))
+
+            for i in range(CHUNKS + 2):
+                block, k = divmod(i, U_PASSES)
+                if 1 <= block <= BLOCKS and k >= 1:
+                    sigmoid_and_turn(block - 1, k - 1)
+                if i < CHUNKS:
+                    regroup_chunk(i)
+                if 1 <= i <= CHUNKS:
+                    quantise_chunk(i - 1)
+                if i == U_PASSES - 3:
+                    small_banks = turn_small_vectors()
+                if i == U_PASSES - 2:
+                    keep_small_vectors(small_banks[0], small_banks[1])
+                    turn_activations()
+                if i == U_PASSES - 1:
+                    quantise_activations()
+                if 1 <= block <= BLOCKS and k == 0:
+                    first_matmul(block - 1)
+                if block >= 2 and k == 0:
+                    blend_block(block - 2)
+
+            blend_sum = work.tile([P, B_TILES], F32, name="blend_sum", tag="blend_sum")
+            nc.vector.tensor_reduce(out=blend_sum[:], in_=blend_sums[:], axis=mybir.AxisListType.X, op=ALU.add)
+            layer_norm(blend, blend_sum[:], H, GAMMA_H_AT, BETA_H_AT, new_h, store_and_turn_new_h)
+
+            out_acc = [psum_acc.tile([P, D], F32, name="out_acc%d" % t, tag="acc") for t in range(B_TILES)]
+            second_matmul(out_acc)
+            pre_out_sum = work.tile([P, B_TILES], F32, name="pre_out_sum", tag="pre_out_sum")
+            for t in range(B_TILES):
+                nc.vector.scalar_tensor_tensor(
+                    out=pre_out[:, t, :], in0=out_acc[t][:], scalar=1.0, in1=bd_all[:],
+                    op0=ALU.mult, op1=ALU.add, accum_out=pre_out_sum[:, t : t + 1],
+                )
+            layer_norm(pre_out, pre_out_sum[:], D, GAMMA_O_AT, BETA_O_AT, out_sb, store_out)

@@ -27,11 +27,12 @@ H_TILES = BANK // P
 WU_CHUNKS = BLOCKS * U_PASSES
 CHUNKS = WU_CHUNKS + D_PASSES
 
-VECTOR_COLS = 192
 RUN = 4
+QUANTISE_LAG = 2
 
-GAMMA_H_AT, BETA_H_AT, B_D_AT, GAMMA_O_AT, BETA_O_AT = 0, H, 2 * H, 2 * H + D, 2 * H + 2 * D
-VEC_COLS = 2 * H + 3 * D
+B_U_AT, GAMMA_H_AT, BETA_H_AT = 0, H // P, 2 * H // P
+B_D_AT, GAMMA_O_AT, BETA_O_AT = 3 * H // P, 3 * H // P + D // P, 3 * H // P + 2 * D // P
+SMALL_COLS = 3 * H // P + 3 * D // P
 
 FLOPS = 2 * B * C * H + 2 * B * H * D
 
@@ -45,46 +46,52 @@ def tile_recurrentffn_pb_kernel(
         raw_pool = ctx.enter_context(tc.tile_pool(name="raw", bufs=8))
         grouped_pool = ctx.enter_context(tc.tile_pool(name="grouped", bufs=4))
         work = ctx.enter_context(tc.tile_pool(name="work", bufs=2))
-        psum_acc = ctx.enter_context(tc.psum_pool(name="psum_acc", bufs=3))
-        psum_turn = ctx.enter_context(tc.psum_pool(name="psum_turn", bufs=3))
+        psum_acc = ctx.enter_context(tc.psum_pool(name="psum_acc", bufs=2))
+        psum_diff = ctx.enter_context(tc.psum_pool(name="psum_diff", bufs=2))
+        psum_turn = ctx.enter_context(tc.psum_pool(name="psum_turn", bufs=2))
         psum_spread = ctx.enter_context(tc.psum_pool(name="psum_spread", bufs=2))
 
         ident = const.tile([P, P], F32, name="ident")
         make_identity(nc, ident[:])
-        ones = const.tile([P, P], BF16, name="ones")
-        nc.vector.memset(ones[:], 1.0)
+        plus_ident = const.tile([P, P], BF16, name="plus_ident")
+        make_identity(nc, plus_ident[:])
+        minus_ident = const.tile([P, P], BF16, name="minus_ident")
+        nc.vector.tensor_scalar_mul(out=minus_ident[:], in0=plus_ident[:], scalar1=-1.0)
         neg_half = const.tile([P, B_TILES], F32, name="neg_half")
         nc.vector.memset(neg_half[:], -0.5)
 
-        bu_loaded = const.tile([H // P, P], BF16, name="bu_loaded")
-        nc.scalar.dma_start(out=bu_loaded[:], in_=b_u.rearrange("(c q) -> c q", q=P))
-        bu_rows = const.tile([P, P], F32, name="bu_rows")
-        nc.vector.memset(bu_rows[:], 0.0)
-        bias_u = const.tile([P, H // P], F32, name="bias_u")
-
-        vec_rows = const.tile([P, VEC_COLS], BF16, name="vec_rows")
-        nc.vector.memset(vec_rows[:], 0.0)
+        small_loaded = const.tile([SMALL_COLS, P], BF16, name="small_loaded")
         for vec, at in (
-            (b_d, B_D_AT), (gamma_h, GAMMA_H_AT), (beta_h, BETA_H_AT), (gamma_o, GAMMA_O_AT), (beta_o, BETA_O_AT)
+            (b_u, B_U_AT), (b_d, B_D_AT), (gamma_h, GAMMA_H_AT), (beta_h, BETA_H_AT),
+            (gamma_o, GAMMA_O_AT), (beta_o, BETA_O_AT),
         ):
             nc.scalar.dma_start(
-                out=vec_rows[0:1, at : at + vec.shape[0]], in_=vec.rearrange("(o n) -> o n", o=1)
+                out=small_loaded[at : at + vec.shape[0] // P, :], in_=vec.rearrange("(c q) -> c q", q=P)
             )
+        small_rows = const.tile([P, P], F32, name="small_rows")
+        nc.vector.memset(small_rows[:], 0.0)
+        small_cols = const.tile([P, SMALL_COLS], F32, name="small_cols")
         bd_all = const.tile([P, D], F32, name="bd_all")
+
+        def turn_small_vectors():
+            nc.vector.tensor_copy(out=small_rows[0:SMALL_COLS, :], in_=small_loaded[:])
+            small_turned = psum_turn.tile([P, P], F32, name="small_turned", tag="turn")
+            nc.tensor.transpose(small_turned[:], small_rows[:], ident[:])
+            return small_turned
+
+        def keep_small_vectors(small_turned):
+            nc.vector.tensor_copy(out=small_cols[:], in_=small_turned[:, 0:SMALL_COLS])
 
         def spread(at):
             bank = psum_spread.tile([P, BANK], F32, name="spread_bank", tag="spread")
-            nc.tensor.matmul(out=bank[:], lhsT=ones[:], rhs=vec_rows[:, at : at + BANK], start=True, stop=True)
+            for c in range(BANK // P):
+                nc.tensor.transpose(
+                    bank[:, c * P : (c + 1) * P], small_cols[:, at + c : at + c + 1].to_broadcast([P, P]), ident[:]
+                )
             return bank
 
-        def turn_small_vectors():
-            nc.vector.tensor_copy(out=bu_rows[0 : H // P, :], in_=bu_loaded[:])
-            bu_turned = psum_turn.tile([P, P], F32, name="bu_turned", tag="turn")
-            nc.tensor.transpose(bu_turned[:], bu_rows[:], ident[:])
-            return bu_turned, spread(B_D_AT)
-
-        def keep_small_vectors(bu_turned, bd_bank):
-            nc.vector.tensor_copy(out=bias_u[:], in_=bu_turned[:, 0 : H // P])
+        def keep_b_d():
+            bd_bank = spread(B_D_AT)
             nc.scalar.copy(out=bd_all[:], in_=bd_bank[:])
 
         wu_codes = const.tile([P, WU_CHUNKS, BANK], U32, name="wu_codes", align_bytes=64)
@@ -109,9 +116,10 @@ def tile_recurrentffn_pb_kernel(
             groupeds.append(grouped_pool.tile([P, BANK, PACK], BF16, name="grouped", tag="grouped", align_bytes=64))
             src = raws[i][:].rearrange("q j (c i) -> q c j i", i=RUN)
             dst = groupeds[i][:].rearrange("q (c i) j -> q c j i", i=RUN)
-            split = VECTOR_COLS // RUN
-            nc.vector.tensor_copy(out=dst[:, :split], in_=src[:, :split])
-            nc.scalar.copy(out=dst[:, split:], in_=src[:, split:])
+            if i % 2 == 0:
+                nc.scalar.copy(out=dst, in_=src)
+            else:
+                nc.vector.tensor_copy(out=dst, in_=src)
 
         def quantise_chunk(i):
             if i < WU_CHUNKS:
@@ -152,71 +160,85 @@ def tile_recurrentffn_pb_kernel(
 
         blend = const.tile([P, B_TILES, H], F32, name="blend")
         blend_sums = const.tile([P, B_TILES, BLOCKS], F32, name="blend_sums")
-        accs, u_banks = [], []
+        accs, diffs, gates, product_banks = [], [], [], []
 
-        def first_matmul(block):
-            for c in range(H_TILES):
-                m_cols = slice(c * P, (c + 1) * P)
-                accs.append(psum_acc.tile([P, B], F32, name="acc", tag="acc"))
-                for g in range(U_PASSES):
-                    nc.tensor.matmul_mx(
-                        out=accs[block * H_TILES + c][:],
-                        lhsT=wu_codes[:, block * U_PASSES + g, m_cols].bitcast(FP8X4),
-                        lhsT_scale=wu_scales[:, block * U_PASSES + g, m_cols],
-                        rhs=comb_codes[:, g, :].bitcast(FP8X4),
-                        rhs_scale=comb_scales[:, g, :],
-                        start=(g == 0),
-                        stop=(g == U_PASSES - 1),
+        def turn_difference(pair):
+            diffs.append(psum_diff.tile([P, 2, B], F32, name="diff", tag="diff"))
+            for half in range(2):
+                feats = slice((2 * pair + half) * P, (2 * pair + half + 1) * P)
+                for t in range(B_TILES):
+                    rows = slice(t * P, (t + 1) * P)
+                    nc.tensor.matmul(
+                        out=diffs[pair][:, half, rows], lhsT=s_sb[:, t, feats], rhs=plus_ident[:], start=True, stop=False
+                    )
+                    nc.tensor.matmul(
+                        out=diffs[pair][:, half, rows], lhsT=h_sb[:, t, feats], rhs=minus_ident[:], start=False, stop=True
                     )
 
-        def sigmoid_and_turn(block, c):
-            feature_tile = block * H_TILES + c
-            u_turned = work.tile([P, B], F32, name="u_turned", tag="u_turned", bufs=4)
-            nc.scalar.activation(
-                out=u_turned[:], in_=accs[feature_tile][:], func=ACT.Sigmoid,
-                bias=bias_u[:, feature_tile : feature_tile + 1], scale=1.0,
-            )
-            for t in range(B_TILES):
-                if c == 0:
-                    u_banks.append(psum_turn.tile([P, BANK], F32, name="u_bank", tag="turn"))
-                nc.tensor.transpose(
-                    u_banks[block * B_TILES + t][:, c * P : (c + 1) * P], u_turned[:, t * P : (t + 1) * P], ident[:]
+        def first_matmul(tile):
+            block, c = divmod(tile, H_TILES)
+            m_cols = slice(c * P, (c + 1) * P)
+            accs.append(psum_acc.tile([P, B], F32, name="acc", tag="acc"))
+            for g in range(U_PASSES):
+                nc.tensor.matmul_mx(
+                    out=accs[tile][:],
+                    lhsT=wu_codes[:, block * U_PASSES + g, m_cols].bitcast(FP8X4),
+                    lhsT_scale=wu_scales[:, block * U_PASSES + g, m_cols],
+                    rhs=comb_codes[:, g, :].bitcast(FP8X4),
+                    rhs_scale=comb_scales[:, g, :],
+                    start=(g == 0),
+                    stop=(g == U_PASSES - 1),
                 )
 
-        def blend_block(block):
-            cols = slice(block * BANK, (block + 1) * BANK)
-            diff = [work.tile([P, BANK], F32, name="diff%d" % t, tag="diff", bufs=4) for t in range(B_TILES)]
+        def sigmoid(tile):
+            gates.append(work.tile([P, B], F32, name="gate", tag="gate", bufs=4))
+            nc.scalar.activation(
+                out=gates[tile][:], in_=accs[tile][:], func=ACT.Sigmoid,
+                bias=small_cols[:, B_U_AT + tile : B_U_AT + tile + 1], scale=1.0,
+            )
+
+        def gate_difference(tile):
+            nc.vector.tensor_tensor(
+                out=gates[tile][:], in0=gates[tile][:], in1=diffs[tile // 2][:, tile % 2, :], op=ALU.mult
+            )
+
+        def turn_product(tile):
+            block, c = divmod(tile, H_TILES)
             for t in range(B_TILES):
-                nc.vector.tensor_tensor(out=diff[t][:], in0=s_sb[:, t, cols], in1=h_sb[:, t, cols], op=ALU.subtract)
-            for t in range(B_TILES):
-                nc.vector.tensor_tensor(
-                    out=diff[t][:], in0=u_banks[block * B_TILES + t][:], in1=diff[t][:], op=ALU.mult
+                if c == 0:
+                    product_banks.append(psum_turn.tile([P, BANK], F32, name="product_bank", tag="turn"))
+                nc.tensor.transpose(
+                    product_banks[block * B_TILES + t][:, c * P : (c + 1) * P], gates[tile][:, t * P : (t + 1) * P], ident[:]
                 )
+
+        def add_hidden(block):
+            cols = slice(block * BANK, (block + 1) * BANK)
             for t in range(B_TILES):
                 nc.vector.scalar_tensor_tensor(
-                    out=blend[:, t, cols], in0=h_sb[:, t, cols], scalar=2.0, in1=diff[t][:],
+                    out=blend[:, t, cols], in0=h_sb[:, t, cols], scalar=2.0, in1=product_banks[block * B_TILES + t][:],
                     op0=ALU.mult, op1=ALU.add, accum_out=blend_sums[:, t, block : block + 1],
                 )
 
         def layer_norm(values, sums, width, gain_at, shift_at, result, after_piece):
             pieces = width // BANK
             neg_mean = work.tile([P, B_TILES], F32, name="neg_mean", tag="neg_mean")
-            nc.vector.tensor_scalar_mul(out=neg_mean[:], in0=sums, scalar1=-1.0 / width)
             sq_sums = work.tile([P, B_TILES], F32, name="sq_sums", tag="sq_sums")
+            var_eps = work.tile([P, B_TILES], F32, name="var_eps", tag="var_eps")
+            rstd = work.tile([P, B_TILES], F32, name="rstd", tag="rstd")
             for t in range(B_TILES):
+                one = slice(t, t + 1)
+                nc.vector.tensor_scalar_mul(out=neg_mean[:, one], in0=sums[:, one], scalar1=-1.0 / width)
                 squares = work.tile([P, width], BF16, name="squares", tag="squares")
                 nc.scalar.activation(
                     out=squares[:], in_=values[:, t, :], func=ACT.Square,
-                    bias=neg_mean[:, t : t + 1], scale=1.0, accum_out=sq_sums[:, t : t + 1],
+                    bias=neg_mean[:, one], scale=1.0, accum_out=sq_sums[:, one],
                 )
-            var_eps = work.tile([P, B_TILES], F32, name="var_eps", tag="var_eps")
-            nc.gpsimd.tensor_scalar(
-                out=var_eps[:], in0=sq_sums[:], scalar1=1.0 / width, scalar2=EPS, op0=ALU.mult, op1=ALU.add
-            )
-            rstd = work.tile([P, B_TILES], F32, name="rstd", tag="rstd")
-            nc.gpsimd.tensor_tensor(out=rstd[:], in0=var_eps[:], in1=neg_half[:], op=ALU.pow)
+                nc.gpsimd.tensor_scalar(
+                    out=var_eps[:, one], in0=sq_sums[:, one], scalar1=1.0 / width, scalar2=EPS, op0=ALU.mult, op1=ALU.add
+                )
+                nc.gpsimd.tensor_tensor(out=rstd[:, one], in0=var_eps[:, one], in1=neg_half[:, one], op=ALU.pow)
 
-            gain = [spread(gain_at + i * BANK) for i in range(min(2, pieces))]
+            gain = [spread(gain_at + i * BANK // P) for i in range(min(2, pieces))]
             for i in range(pieces):
                 cols = slice(i * BANK, (i + 1) * BANK)
                 for t in range(B_TILES):
@@ -225,8 +247,8 @@ def tile_recurrentffn_pb_kernel(
                         op0=ALU.add, op1=ALU.mult,
                     )
                 if i + 2 < pieces:
-                    gain.append(spread(gain_at + (i + 2) * BANK))
-            shift = [spread(shift_at + i * BANK) for i in range(min(2, pieces))]
+                    gain.append(spread(gain_at + (i + 2) * BANK // P))
+            shift = [spread(shift_at + i * BANK // P) for i in range(min(2, pieces))]
             for i in range(pieces):
                 cols = slice(i * BANK, (i + 1) * BANK)
                 for t in range(B_TILES):
@@ -234,24 +256,23 @@ def tile_recurrentffn_pb_kernel(
                         out=result[:, t, cols], in0=result[:, t, cols], scalar=rstd[:, t : t + 1], in1=shift[i][:],
                         op0=ALU.mult, op1=ALU.add,
                     )
+                    after_piece(i, t)
                 if i + 2 < pieces:
-                    shift.append(spread(shift_at + (i + 2) * BANK))
-                after_piece(i)
+                    shift.append(spread(shift_at + (i + 2) * BANK // P))
 
         new_h = const.tile([P, B_TILES, H], F32, name="new_h")
         nh_grouped = const.tile([P, D_PASSES, B, PACK], BF16, name="nh_grouped", align_bytes=64)
         nh_codes = const.tile([P, D_PASSES, B], U32, name="nh_codes", align_bytes=64)
         nh_scales = const.tile([P, D_PASSES, B], U8, name="nh_scales", align_bytes=64)
 
-        def store_and_turn_new_h(g):
-            cols = slice(g * K_PASS, (g + 1) * K_PASS)
-            nc.sync.dma_start(out=out_1.rearrange("(t r) k -> r t k", r=P)[:, :, cols], in_=new_h[:, :, cols])
-            for t in range(B_TILES):
-                turned = psum_turn.tile([P, PACK, P], F32, name="turned", tag="turn")
-                for j in range(PACK):
-                    k0 = g * K_PASS + j * P
-                    nc.tensor.transpose(turned[:, j, :], new_h[:, t, k0 : k0 + P], ident[:])
-                nc.scalar.copy(out=nh_grouped[:, g, t * P : (t + 1) * P, :], in_=turned[:].rearrange("q j r -> q r j"))
+        def store_and_turn_new_h(g, t):
+            rows = slice(t * P, (t + 1) * P)
+            nc.sync.dma_start(out=out_1[rows, g * K_PASS : (g + 1) * K_PASS], in_=new_h[:, t, g * K_PASS : (g + 1) * K_PASS])
+            turned = psum_turn.tile([P, PACK, P], F32, name="turned", tag="turn")
+            for j in range(PACK):
+                k0 = g * K_PASS + j * P
+                nc.tensor.transpose(turned[:, j, :], new_h[:, t, k0 : k0 + P], ident[:])
+            nc.scalar.copy(out=nh_grouped[:, g, rows, :], in_=turned[:].rearrange("q j r -> q r j"))
 
         def second_matmul(out_acc):
             for g in range(D_PASSES):
@@ -275,8 +296,8 @@ def tile_recurrentffn_pb_kernel(
         pre_out = const.tile([P, B_TILES, D], F32, name="pre_out")
         out_sb = const.tile([P, B_TILES, D], F32, name="out_sb")
 
-        def store_out(piece):
-            nc.sync.dma_start(out=out_0.rearrange("(t r) n -> r t n", r=P), in_=out_sb[:])
+        def store_out(piece, t):
+            nc.sync.dma_start(out=out_0[t * P : (t + 1) * P, :], in_=out_sb[:, t, :])
 
         with tc.manual_schedule():
             for i in range(CHUNKS):
@@ -287,25 +308,36 @@ def tile_recurrentffn_pb_kernel(
                 if i == U_PASSES - 1:
                     nc.sync.dma_start(out=s_sb[:], in_=swiglu.rearrange("(t r) k -> r t k", r=P))
 
-            for i in range(CHUNKS + 2):
-                block, k = divmod(i, U_PASSES)
-                if 1 <= block <= BLOCKS and k >= 1:
-                    sigmoid_and_turn(block - 1, k - 1)
+            def entering(r):
+                block, c = divmod(r - (U_PASSES - 1 + QUANTISE_LAG), U_PASSES)
+                return block * H_TILES + c if 0 <= block < BLOCKS and c < H_TILES else None
+
+            for i in range(CHUNKS + QUANTISE_LAG + 3):
+                if entering(i - 1) is not None:
+                    sigmoid(entering(i - 1))
+                if entering(i - 3) is not None:
+                    turn_product(entering(i - 3))
                 if i < CHUNKS:
                     regroup_chunk(i)
-                if 1 <= i <= CHUNKS:
-                    quantise_chunk(i - 1)
-                if i == U_PASSES - 3:
-                    small_banks = turn_small_vectors()
+                if 0 <= i - QUANTISE_LAG < CHUNKS:
+                    quantise_chunk(i - QUANTISE_LAG)
+                if i == 1:
+                    small_turned = turn_small_vectors()
+                if i == 2:
+                    keep_small_vectors(small_turned)
                 if i == U_PASSES - 2:
-                    keep_small_vectors(small_banks[0], small_banks[1])
+                    keep_b_d()
                     turn_activations()
                 if i == U_PASSES - 1:
                     quantise_activations()
-                if 1 <= block <= BLOCKS and k == 0:
-                    first_matmul(block - 1)
-                if block >= 2 and k == 0:
-                    blend_block(block - 2)
+                if entering(i - 4) is not None and entering(i - 4) % H_TILES == H_TILES - 1:
+                    add_hidden(entering(i - 4) // H_TILES)
+                if entering(i - 2) is not None:
+                    gate_difference(entering(i - 2))
+                if entering(i - 1) is not None and entering(i - 1) % 2 == 0:
+                    turn_difference(entering(i - 1) // 2)
+                if entering(i) is not None:
+                    first_matmul(entering(i))
 
             blend_sum = work.tile([P, B_TILES], F32, name="blend_sum", tag="blend_sum")
             nc.vector.tensor_reduce(out=blend_sum[:], in_=blend_sums[:], axis=mybir.AxisListType.X, op=ALU.add)

@@ -305,8 +305,9 @@ def tile_recurrentffn_pb_kernel(
                 if i == 1:
                     nc.sync.dma_start(out=x_sb[:], in_=x.rearrange("(t r) k -> r t k", r=P))
                     nc.sync.dma_start(out=h_sb[:], in_=hidden_state.rearrange("(t r) k -> r t k", r=P))
-                if i == U_PASSES - 1:
-                    nc.sync.dma_start(out=s_sb[:], in_=swiglu.rearrange("(t r) k -> r t k", r=P))
+                if i < WU_CHUNKS and i % U_PASSES == U_PASSES - 1:
+                    cols = slice(i // U_PASSES * BANK, (i // U_PASSES + 1) * BANK)
+                    nc.sync.dma_start(out=s_sb[:, :, cols], in_=swiglu.rearrange("(t r) k -> r t k", r=P)[:, :, cols])
 
             def entering(r):
                 block, c = divmod(r - (U_PASSES - 1 + QUANTISE_LAG), U_PASSES)

@@ -24,15 +24,13 @@ U_PASSES = C // K_PASS
 D_PASSES = H // K_PASS
 BLOCKS = H // BANK
 H_TILES = BANK // P
+PAIRS = H_TILES // 2
 WU_CHUNKS = BLOCKS * U_PASSES
 CHUNKS = WU_CHUNKS + D_PASSES
+BU_COLS = H // P
 
 RUN = 4
 QUANTISE_LAG = 2
-
-B_U_AT, GAMMA_H_AT, BETA_H_AT = 0, H // P, 2 * H // P
-B_D_AT, GAMMA_O_AT, BETA_O_AT = 3 * H // P, 3 * H // P + D // P, 3 * H // P + 2 * D // P
-SMALL_COLS = 3 * H // P + 3 * D // P
 
 FLOPS = 2 * B * C * H + 2 * B * H * D
 
@@ -46,10 +44,9 @@ def tile_recurrentffn_pb_kernel(
         raw_pool = ctx.enter_context(tc.tile_pool(name="raw", bufs=8))
         grouped_pool = ctx.enter_context(tc.tile_pool(name="grouped", bufs=4))
         work = ctx.enter_context(tc.tile_pool(name="work", bufs=2))
-        psum_acc = ctx.enter_context(tc.psum_pool(name="psum_acc", bufs=2))
+        psum_acc = ctx.enter_context(tc.psum_pool(name="psum_acc", bufs=4))
         psum_diff = ctx.enter_context(tc.psum_pool(name="psum_diff", bufs=2))
         psum_turn = ctx.enter_context(tc.psum_pool(name="psum_turn", bufs=2))
-        psum_spread = ctx.enter_context(tc.psum_pool(name="psum_spread", bufs=2))
 
         ident = const.tile([P, P], F32, name="ident")
         make_identity(nc, ident[:])
@@ -60,45 +57,28 @@ def tile_recurrentffn_pb_kernel(
         neg_half = const.tile([P, B_TILES], F32, name="neg_half")
         nc.vector.memset(neg_half[:], -0.5)
 
-        small_loaded = const.tile([SMALL_COLS, P], BF16, name="small_loaded")
-        for vec, at in (
-            (b_u, B_U_AT), (b_d, B_D_AT), (gamma_h, GAMMA_H_AT), (beta_h, BETA_H_AT),
-            (gamma_o, GAMMA_O_AT), (beta_o, BETA_O_AT),
-        ):
-            nc.scalar.dma_start(
-                out=small_loaded[at : at + vec.shape[0] // P, :], in_=vec.rearrange("(c q) -> c q", q=P)
-            )
-        small_rows = const.tile([P, P], F32, name="small_rows")
-        nc.vector.memset(small_rows[:], 0.0)
-        small_cols = const.tile([P, SMALL_COLS], F32, name="small_cols")
-        bd_all = const.tile([P, D], F32, name="bd_all")
+        warm = const.tile([P, 1], F32, name="warm")
+        nc.scalar.activation(out=warm[:], in_=neg_half[:, 0:1], func=ACT.Sigmoid)
 
-        def turn_small_vectors():
-            nc.vector.tensor_copy(out=small_rows[0:SMALL_COLS, :], in_=small_loaded[:])
-            small_turned = psum_turn.tile([P, P], F32, name="small_turned", tag="turn")
-            nc.tensor.transpose(small_turned[:], small_rows[:], ident[:])
-            return small_turned
+        bu_rows = const.tile([P, P], BF16, name="bu_rows")
+        nc.vector.memset(bu_rows[:], 0.0)
+        bu_cols = const.tile([P, BU_COLS], F32, name="bu_cols")
+        gamma_h_all = const.tile([P, H], BF16, name="gamma_h_all")
+        beta_h_all = const.tile([P, H], BF16, name="beta_h_all")
+        b_d_all = const.tile([P, D], BF16, name="b_d_all")
+        gamma_o_all = const.tile([P, D], BF16, name="gamma_o_all")
+        beta_o_all = const.tile([P, D], BF16, name="beta_o_all")
 
-        def keep_small_vectors(small_turned):
-            nc.vector.tensor_copy(out=small_cols[:], in_=small_turned[:, 0:SMALL_COLS])
-
-        def spread(at):
-            bank = psum_spread.tile([P, BANK], F32, name="spread_bank", tag="spread")
-            for c in range(BANK // P):
-                nc.tensor.transpose(
-                    bank[:, c * P : (c + 1) * P], small_cols[:, at + c : at + c + 1].to_broadcast([P, P]), ident[:]
-                )
-            return bank
-
-        def keep_b_d():
-            bd_bank = spread(B_D_AT)
-            nc.scalar.copy(out=bd_all[:], in_=bd_bank[:])
+        def turn_b_u():
+            turned = psum_turn.tile([P, P], BF16, name="bu_turned", tag="turn")
+            nc.tensor.transpose(turned[:], bu_rows[:], plus_ident[:])
+            return turned
 
         wu_codes = const.tile([P, WU_CHUNKS, BANK], U32, name="wu_codes", align_bytes=64)
         wu_scales = const.tile([P, WU_CHUNKS, BANK], U8, name="wu_scales", align_bytes=64)
         wd_codes = const.tile([P, D_PASSES, D], U32, name="wd_codes", align_bytes=64)
         wd_scales = const.tile([P, D_PASSES, D], U8, name="wd_scales", align_bytes=64)
-        raws, groupeds = [], []
+        raws, groupeds = [], {}
 
         def load_chunk(i):
             if i < WU_CHUNKS:
@@ -112,11 +92,11 @@ def tile_recurrentffn_pb_kernel(
             raws.append(raw_pool.tile([P, PACK, BANK], BF16, name="raw", tag="raw"))
             nc.sync.dma_start(out=raws[i][:], in_=view)
 
-        def regroup_chunk(i):
-            groupeds.append(grouped_pool.tile([P, BANK, PACK], BF16, name="grouped", tag="grouped", align_bytes=64))
+        def regroup_chunk(i, on_scalar):
+            groupeds[i] = grouped_pool.tile([P, BANK, PACK], BF16, name="grouped", tag="grouped", align_bytes=64)
             src = raws[i][:].rearrange("q j (c i) -> q c j i", i=RUN)
             dst = groupeds[i][:].rearrange("q (c i) j -> q c j i", i=RUN)
-            if i % 2 == 0:
+            if on_scalar:
                 nc.scalar.copy(out=dst, in_=src)
             else:
                 nc.vector.tensor_copy(out=dst, in_=src)
@@ -137,219 +117,298 @@ def tile_recurrentffn_pb_kernel(
         comb_codes = const.tile([P, U_PASSES, B], U32, name="comb_codes", align_bytes=64)
         comb_scales = const.tile([P, U_PASSES, B], U8, name="comb_scales", align_bytes=64)
 
-        def turn_activations():
-            for g in range(U_PASSES):
-                turned = psum_turn.tile([P, 2, B], F32, name="turned", tag="turn")
-                for t in range(B_TILES):
-                    feats = x_sb[:, t, :] if g == 0 else h_sb[:, t, (g - 1) * K_PASS : g * K_PASS]
-                    words = feats.bitcast(F32).rearrange("r (q u) -> r u q", u=2)
-                    for u in range(2):
-                        nc.tensor.transpose(turned[:, u, t * P : (t + 1) * P], words[:, u, :], ident[:])
-                nc.scalar.copy(
-                    out=comb_grouped[:, g].rearrange("q r j -> q (r j)").bitcast(F32).rearrange("q (r u) -> q r u", u=2),
-                    in_=turned[:].rearrange("q u r -> q r u"),
-                )
+        def turn_activations(g):
+            turned = psum_turn.tile([P, 2, B], F32, name="turned", tag="turn")
+            for t in range(B_TILES):
+                feats = x_sb[:, t, :] if g == 0 else h_sb[:, t, (g - 1) * K_PASS : g * K_PASS]
+                words = feats.bitcast(F32).rearrange("r (q u) -> r u q", u=2)
+                for u in range(2):
+                    nc.tensor.transpose(turned[:, u, t * P : (t + 1) * P], words[:, u, :], ident[:])
+            nc.scalar.copy(
+                out=comb_grouped[:, g].rearrange("q r j -> q (r j)").bitcast(F32).rearrange("q (r u) -> q r u", u=2),
+                in_=turned[:].rearrange("q u r -> q r u"),
+            )
 
-        def quantise_activations():
-            for g in range(U_PASSES):
-                nc.vector.quantize_mx(
-                    out=comb_codes[:, g, :].bitcast(FP8X4),
-                    scales=comb_scales[:, g, :],
-                    in_=comb_grouped[:, g].rearrange("q r j -> q (r j)"),
-                )
+        def quantise_activations(g):
+            nc.vector.quantize_mx(
+                out=comb_codes[:, g, :].bitcast(FP8X4),
+                scales=comb_scales[:, g, :],
+                in_=comb_grouped[:, g].rearrange("q r j -> q (r j)"),
+            )
 
         blend = const.tile([P, B_TILES, H], F32, name="blend")
-        blend_sums = const.tile([P, B_TILES, BLOCKS], F32, name="blend_sums")
-        accs, diffs, gates, product_banks = [], [], [], []
+        blend_sums = const.tile([P, BLOCKS, B_TILES], F32, name="blend_sums")
+        sq_sums = const.tile([P, BLOCKS, B_TILES], F32, name="sq_sums")
+        neg_centre = const.tile([P, B_TILES], F32, name="neg_centre")
+        accs, diffs, gates, product_banks = {}, {}, {}, {}
 
-        def turn_difference(pair):
-            diffs.append(psum_diff.tile([P, 2, B], F32, name="diff", tag="diff"))
+        def turn_difference(block, pair):
+            diff = psum_diff.tile([P, 2, B], F32, name="diff", tag="diff")
+            diffs[block, pair] = diff
             for half in range(2):
-                feats = slice((2 * pair + half) * P, (2 * pair + half + 1) * P)
+                first = block * BANK + (2 * pair + half) * P
                 for t in range(B_TILES):
                     rows = slice(t * P, (t + 1) * P)
                     nc.tensor.matmul(
-                        out=diffs[pair][:, half, rows], lhsT=s_sb[:, t, feats], rhs=plus_ident[:], start=True, stop=False
+                        out=diff[:, half, rows], lhsT=s_sb[:, t, first : first + P], rhs=plus_ident[:], start=True, stop=False
                     )
                     nc.tensor.matmul(
-                        out=diffs[pair][:, half, rows], lhsT=h_sb[:, t, feats], rhs=minus_ident[:], start=False, stop=True
+                        out=diff[:, half, rows], lhsT=h_sb[:, t, first : first + P], rhs=minus_ident[:], start=False, stop=True
                     )
 
-        def first_matmul(tile):
-            block, c = divmod(tile, H_TILES)
-            m_cols = slice(c * P, (c + 1) * P)
-            accs.append(psum_acc.tile([P, B], F32, name="acc", tag="acc"))
-            for g in range(U_PASSES):
+        def first_matmul(i):
+            block, g = divmod(i, U_PASSES)
+            for c in range(H_TILES):
+                if g == 0:
+                    accs[block, c] = psum_acc.tile([P, BANK], F32, name="acc", tag="acc")
+                m_cols = slice(c * P, (c + 1) * P)
                 nc.tensor.matmul_mx(
-                    out=accs[tile][:],
-                    lhsT=wu_codes[:, block * U_PASSES + g, m_cols].bitcast(FP8X4),
-                    lhsT_scale=wu_scales[:, block * U_PASSES + g, m_cols],
+                    out=accs[block, c][:, 0:B],
+                    lhsT=wu_codes[:, i, m_cols].bitcast(FP8X4),
+                    lhsT_scale=wu_scales[:, i, m_cols],
                     rhs=comb_codes[:, g, :].bitcast(FP8X4),
                     rhs_scale=comb_scales[:, g, :],
                     start=(g == 0),
                     stop=(g == U_PASSES - 1),
                 )
 
-        def sigmoid(tile):
-            gates.append(work.tile([P, B], F32, name="gate", tag="gate", bufs=4))
-            nc.scalar.activation(
-                out=gates[tile][:], in_=accs[tile][:], func=ACT.Sigmoid,
-                bias=small_cols[:, B_U_AT + tile : B_U_AT + tile + 1], scale=1.0,
-            )
-
-        def gate_difference(tile):
-            nc.vector.tensor_tensor(
-                out=gates[tile][:], in0=gates[tile][:], in1=diffs[tile // 2][:, tile % 2, :], op=ALU.mult
-            )
-
-        def turn_product(tile):
-            block, c = divmod(tile, H_TILES)
-            for t in range(B_TILES):
-                if c == 0:
-                    product_banks.append(psum_turn.tile([P, BANK], F32, name="product_bank", tag="turn"))
-                nc.tensor.transpose(
-                    product_banks[block * B_TILES + t][:, c * P : (c + 1) * P], gates[tile][:, t * P : (t + 1) * P], ident[:]
+        def sigmoid(block, pair):
+            gate = work.tile([P, 2, B], F32, name="gate", tag="gate")
+            gates[block, pair] = gate
+            for half in range(2):
+                c = 2 * pair + half
+                tile = block * H_TILES + c
+                nc.scalar.activation(
+                    out=gate[:, half, :], in_=accs[block, c][:, 0:B], func=ACT.Sigmoid,
+                    bias=bu_cols[:, tile : tile + 1], scale=1.0,
                 )
+
+        def gate_difference(block, pair):
+            gate = gates[block, pair]
+            nc.vector.tensor_tensor(out=gate[:], in0=gate[:], in1=diffs[block, pair][:], op=ALU.mult)
+
+        def turn_product(block, pair):
+            for t in range(B_TILES):
+                if pair == 0:
+                    product_banks[block, t] = psum_turn.tile([P, BANK], F32, name="product_bank", tag="turn")
+                for half in range(2):
+                    c = 2 * pair + half
+                    nc.tensor.transpose(
+                        product_banks[block, t][:, c * P : (c + 1) * P], gates[block, pair][:, half, t * P : (t + 1) * P], ident[:]
+                    )
 
         def add_hidden(block):
             cols = slice(block * BANK, (block + 1) * BANK)
             for t in range(B_TILES):
                 nc.vector.scalar_tensor_tensor(
-                    out=blend[:, t, cols], in0=h_sb[:, t, cols], scalar=2.0, in1=product_banks[block * B_TILES + t][:],
-                    op0=ALU.mult, op1=ALU.add, accum_out=blend_sums[:, t, block : block + 1],
+                    out=blend[:, t, cols], in0=h_sb[:, t, cols], scalar=2.0, in1=product_banks[block, t][:],
+                    op0=ALU.mult, op1=ALU.add, accum_out=blend_sums[:, block, t : t + 1],
                 )
+            if block == 0:
+                nc.vector.tensor_scalar_mul(out=neg_centre[:], in0=blend_sums[:, 0, :], scalar1=-1.0 / BANK)
 
-        def layer_norm(values, sums, width, gain_at, shift_at, result, after_piece):
-            pieces = width // BANK
-            neg_mean = work.tile([P, B_TILES], F32, name="neg_mean", tag="neg_mean")
-            sq_sums = work.tile([P, B_TILES], F32, name="sq_sums", tag="sq_sums")
-            var_eps = work.tile([P, B_TILES], F32, name="var_eps", tag="var_eps")
-            rstd = work.tile([P, B_TILES], F32, name="rstd", tag="rstd")
+        def square_sums(block):
+            cols = slice(block * BANK, (block + 1) * BANK)
             for t in range(B_TILES):
-                one = slice(t, t + 1)
-                nc.vector.tensor_scalar_mul(out=neg_mean[:, one], in0=sums[:, one], scalar1=-1.0 / width)
-                squares = work.tile([P, width], BF16, name="squares", tag="squares")
+                squares = work.tile([P, BANK], BF16, name="squares", tag="squares")
                 nc.scalar.activation(
-                    out=squares[:], in_=values[:, t, :], func=ACT.Square,
-                    bias=neg_mean[:, one], scale=1.0, accum_out=sq_sums[:, one],
+                    out=squares[:], in_=blend[:, t, cols], func=ACT.Square,
+                    bias=neg_centre[:, t : t + 1], scale=1.0, accum_out=sq_sums[:, block, t : t + 1],
                 )
-                nc.gpsimd.tensor_scalar(
-                    out=var_eps[:, one], in0=sq_sums[:, one], scalar1=1.0 / width, scalar2=EPS, op0=ALU.mult, op1=ALU.add
-                )
-                nc.gpsimd.tensor_tensor(out=rstd[:, one], in0=var_eps[:, one], in1=neg_half[:, one], op=ALU.pow)
-
-            gain = [spread(gain_at + i * BANK // P) for i in range(min(2, pieces))]
-            for i in range(pieces):
-                cols = slice(i * BANK, (i + 1) * BANK)
-                for t in range(B_TILES):
-                    nc.vector.scalar_tensor_tensor(
-                        out=result[:, t, cols], in0=values[:, t, cols], scalar=neg_mean[:, t : t + 1], in1=gain[i][:],
-                        op0=ALU.add, op1=ALU.mult,
-                    )
-                if i + 2 < pieces:
-                    gain.append(spread(gain_at + (i + 2) * BANK // P))
-            shift = [spread(shift_at + i * BANK // P) for i in range(min(2, pieces))]
-            for i in range(pieces):
-                cols = slice(i * BANK, (i + 1) * BANK)
-                for t in range(B_TILES):
-                    nc.vector.scalar_tensor_tensor(
-                        out=result[:, t, cols], in0=result[:, t, cols], scalar=rstd[:, t : t + 1], in1=shift[i][:],
-                        op0=ALU.mult, op1=ALU.add,
-                    )
-                    after_piece(i, t)
-                if i + 2 < pieces:
-                    shift.append(spread(shift_at + (i + 2) * BANK // P))
 
         new_h = const.tile([P, B_TILES, H], F32, name="new_h")
-        nh_grouped = const.tile([P, D_PASSES, B, PACK], BF16, name="nh_grouped", align_bytes=64)
-        nh_codes = const.tile([P, D_PASSES, B], U32, name="nh_codes", align_bytes=64)
-        nh_scales = const.tile([P, D_PASSES, B], U8, name="nh_scales", align_bytes=64)
+        nh_grouped = const.tile([P, B_TILES, D_PASSES, P, PACK], BF16, name="nh_grouped", align_bytes=64)
+        nh_codes = const.tile([P, B_TILES, D_PASSES, P], U32, name="nh_codes", align_bytes=64)
+        nh_scales = const.tile([P, B_TILES, D_PASSES, P], U8, name="nh_scales", align_bytes=64)
+        neg_mean = const.tile([P, B_TILES], F32, name="neg_mean")
+        rstd = const.tile([P, B_TILES], F32, name="rstd")
+        GAIN_COLS = 2 * BANK
 
-        def store_and_turn_new_h(g, t):
-            rows = slice(t * P, (t + 1) * P)
-            nc.sync.dma_start(out=out_1[rows, g * K_PASS : (g + 1) * K_PASS], in_=new_h[:, t, g * K_PASS : (g + 1) * K_PASS])
-            turned = psum_turn.tile([P, PACK, P], F32, name="turned", tag="turn")
+        def apply_gain(t, piece):
+            cols = slice(piece * GAIN_COLS, (piece + 1) * GAIN_COLS)
+            nc.vector.scalar_tensor_tensor(
+                out=new_h[:, t, cols], in0=blend[:, t, cols], scalar=neg_mean[:, t : t + 1], in1=gamma_h_all[:, cols],
+                op0=ALU.add, op1=ALU.mult,
+            )
+
+        def apply_shift(t, g):
+            cols = slice(g * K_PASS, (g + 1) * K_PASS)
+            nc.vector.scalar_tensor_tensor(
+                out=new_h[:, t, cols], in0=new_h[:, t, cols], scalar=rstd[:, t : t + 1], in1=beta_h_all[:, cols],
+                op0=ALU.mult, op1=ALU.add,
+            )
+            nc.sync.dma_start(out=out_1[t * P : (t + 1) * P, cols], in_=new_h[:, t, cols])
+            pool, tag = (psum_turn, "turn") if g % 2 == 0 else (psum_diff, "diff")
+            turned = pool.tile([P, PACK, P], F32, name="nh_turned", tag=tag)
             for j in range(PACK):
                 k0 = g * K_PASS + j * P
                 nc.tensor.transpose(turned[:, j, :], new_h[:, t, k0 : k0 + P], ident[:])
-            nc.scalar.copy(out=nh_grouped[:, g, rows, :], in_=turned[:].rearrange("q j r -> q r j"))
+            nc.scalar.copy(out=nh_grouped[:, t, g], in_=turned[:].rearrange("q j r -> q r j"))
 
-        def second_matmul(out_acc):
-            for g in range(D_PASSES):
-                nc.vector.quantize_mx(
-                    out=nh_codes[:, g, :].bitcast(FP8X4),
-                    scales=nh_scales[:, g, :],
-                    in_=nh_grouped[:, g].rearrange("q r j -> q (r j)"),
+        def quantise_new_h(t, first, last):
+            nc.vector.quantize_mx(
+                out=nh_codes[:, t, first:last].rearrange("q g r -> q (g r)").bitcast(FP8X4),
+                scales=nh_scales[:, t, first:last].rearrange("q g r -> q (g r)"),
+                in_=nh_grouped[:, t, first:last].rearrange("q g r j -> q (g r j)"),
+            )
+
+        out_acc = {}
+
+        def second_matmul(t, first, last):
+            if first == 0:
+                out_acc[t] = psum_acc.tile([P, D], F32, name="out_acc", tag="acc")
+            for g in range(first, last):
+                nc.tensor.matmul_mx(
+                    out=out_acc[t][:],
+                    lhsT=nh_codes[:, t, g, :].bitcast(FP8X4),
+                    lhsT_scale=nh_scales[:, t, g, :],
+                    rhs=wd_codes[:, g, :].bitcast(FP8X4),
+                    rhs_scale=wd_scales[:, g, :],
+                    start=(g == 0),
+                    stop=(g == D_PASSES - 1),
                 )
-                for t in range(B_TILES):
-                    rows = slice(t * P, (t + 1) * P)
-                    nc.tensor.matmul_mx(
-                        out=out_acc[t][:],
-                        lhsT=nh_codes[:, g, rows].bitcast(FP8X4),
-                        lhsT_scale=nh_scales[:, g, rows],
-                        rhs=wd_codes[:, g, :].bitcast(FP8X4),
-                        rhs_scale=wd_scales[:, g, :],
-                        start=(g == 0),
-                        stop=(g == D_PASSES - 1),
-                    )
 
         pre_out = const.tile([P, B_TILES, D], F32, name="pre_out")
         out_sb = const.tile([P, B_TILES, D], F32, name="out_sb")
+        out_stats = [[work.tile([P, 1], F32, name="out_%s%d" % (what, t)) for what in ("sum", "mean", "sq", "var", "rstd")] for t in range(B_TILES)]
 
-        def store_out(piece, t):
+        def output_sums(t):
+            total, neg, sq, var, rs = out_stats[t]
+            nc.vector.scalar_tensor_tensor(
+                out=pre_out[:, t, :], in0=out_acc[t][:], scalar=1.0, in1=b_d_all[:],
+                op0=ALU.mult, op1=ALU.add, accum_out=total[:],
+            )
+            nc.vector.tensor_scalar_mul(out=neg[:], in0=total[:], scalar1=-1.0 / D)
+            squares = work.tile([P, BANK], BF16, name="squares", tag="squares")
+            nc.scalar.activation(
+                out=squares[:], in_=pre_out[:, t, :], func=ACT.Square, bias=neg[:], scale=1.0, accum_out=sq[:]
+            )
+            nc.gpsimd.tensor_scalar(out=var[:], in0=sq[:], scalar1=1.0 / D, scalar2=EPS, op0=ALU.mult, op1=ALU.add)
+            nc.gpsimd.tensor_tensor(out=rs[:], in0=var[:], in1=neg_half[:, 0:1], op=ALU.pow)
+            nc.vector.scalar_tensor_tensor(
+                out=out_sb[:, t, :], in0=pre_out[:, t, :], scalar=neg[:], in1=gamma_o_all[:], op0=ALU.add, op1=ALU.mult
+            )
+
+        def output_shift(t):
+            nc.vector.scalar_tensor_tensor(
+                out=out_sb[:, t, :], in0=out_sb[:, t, :], scalar=out_stats[t][4][:], in1=beta_o_all[:],
+                op0=ALU.mult, op1=ALU.add,
+            )
             nc.sync.dma_start(out=out_0[t * P : (t + 1) * P, :], in_=out_sb[:, t, :])
 
         with tc.manual_schedule():
+            by_tile = lambda dram: dram.rearrange("(t r) k -> r t k", r=P)
             for i in range(CHUNKS):
                 load_chunk(i)
                 if i == 1:
-                    nc.sync.dma_start(out=x_sb[:], in_=x.rearrange("(t r) k -> r t k", r=P))
-                    nc.sync.dma_start(out=h_sb[:], in_=hidden_state.rearrange("(t r) k -> r t k", r=P))
+                    nc.sync.dma_start(out=x_sb[:], in_=by_tile(x))
+                if 1 <= i <= BLOCKS:
+                    cols = slice((i - 1) * BANK, i * BANK)
+                    nc.sync.dma_start(out=h_sb[:, :, cols], in_=by_tile(hidden_state)[:, :, cols])
+                if i == 2:
+                    nc.sync.dma_start(out=bu_rows[0:BU_COLS, :], in_=b_u.rearrange("(c q) -> c q", q=P))
                 if i < WU_CHUNKS and i % U_PASSES == U_PASSES - 1:
                     cols = slice(i // U_PASSES * BANK, (i // U_PASSES + 1) * BANK)
-                    nc.sync.dma_start(out=s_sb[:, :, cols], in_=swiglu.rearrange("(t r) k -> r t k", r=P)[:, :, cols])
+                    nc.sync.dma_start(out=s_sb[:, :, cols], in_=by_tile(swiglu)[:, :, cols])
+            for vec, tile in (
+                (gamma_h, gamma_h_all), (beta_h, beta_h_all), (b_d, b_d_all), (gamma_o, gamma_o_all), (beta_o, beta_o_all)
+            ):
+                nc.sync.dma_start(out=tile[:], in_=vec.partition_broadcast(P))
 
-            def entering(r):
-                block, c = divmod(r - (U_PASSES - 1 + QUANTISE_LAG), U_PASSES)
-                return block * H_TILES + c if 0 <= block < BLOCKS and c < H_TILES else None
-
-            for i in range(CHUNKS + QUANTISE_LAG + 3):
-                if entering(i - 1) is not None:
-                    sigmoid(entering(i - 1))
-                if entering(i - 3) is not None:
-                    turn_product(entering(i - 3))
-                if i < CHUNKS:
-                    regroup_chunk(i)
-                if 0 <= i - QUANTISE_LAG < CHUNKS:
+            FIRST_END = U_PASSES - 1 + QUANTISE_LAG
+            last_round = FIRST_END + BLOCKS * U_PASSES
+            for i in range(last_round + 1):
+                block, since = divmod(i - FIRST_END, U_PASSES)
+                live = 0 <= block < BLOCKS
+                if live and since in (1, 2):
+                    sigmoid(block, since - 1)
+                if live and since in (3, 4):
+                    turn_product(block, since - 3)
+                if since == 2 and 1 <= block < BLOCKS:
+                    square_sums(block - 1)
+                if i < WU_CHUNKS:
+                    regroup_chunk(i, on_scalar=(i % 2 == 0))
+                if i == WU_CHUNKS:
+                    regroup_chunk(WU_CHUNKS, on_scalar=True)
+                if 0 <= i - QUANTISE_LAG < WU_CHUNKS:
                     quantise_chunk(i - QUANTISE_LAG)
-                if i == 1:
-                    small_turned = turn_small_vectors()
-                if i == 2:
-                    keep_small_vectors(small_turned)
-                if i == U_PASSES - 2:
-                    keep_b_d()
-                    turn_activations()
-                if i == U_PASSES - 1:
-                    quantise_activations()
-                if entering(i - 4) is not None and entering(i - 4) % H_TILES == H_TILES - 1:
-                    add_hidden(entering(i - 4) // H_TILES)
-                if entering(i - 2) is not None:
-                    gate_difference(entering(i - 2))
-                if entering(i - 1) is not None and entering(i - 1) % 2 == 0:
-                    turn_difference(entering(i - 1) // 2)
-                if entering(i) is not None:
-                    first_matmul(entering(i))
+                if i == WU_CHUNKS + 2:
+                    regroup_chunk(WU_CHUNKS + 1, on_scalar=False)
+                if 1 <= i <= U_PASSES:
+                    turn_activations(i - 1)
+                if 2 <= i <= U_PASSES + 1:
+                    quantise_activations(i - 2)
+                if i == U_PASSES:
+                    bu_turned = turn_b_u()
+                if i == U_PASSES + 1:
+                    nc.vector.tensor_copy(out=bu_cols[:], in_=bu_turned[:, 0:BU_COLS])
+                if i == last_round:
+                    quantise_chunk(WU_CHUNKS)
+                if since == 0 and 1 <= block <= BLOCKS:
+                    add_hidden(block - 1)
+                if live and since in (2, 3):
+                    gate_difference(block, since - 2)
+                if 0 <= i - QUANTISE_LAG < WU_CHUNKS:
+                    first_matmul(i - QUANTISE_LAG)
+                ahead, left = divmod(i - FIRST_END + 2, U_PASSES)
+                if 0 <= ahead < BLOCKS and left < PAIRS:
+                    turn_difference(ahead, left)
+                if i == last_round - 1:
+                    part_sum = work.tile([P, B_TILES], F32, name="part_sum")
+                    nc.vector.tensor_reduce(
+                        out=part_sum[:], in_=blend_sums[:, 0 : BLOCKS - 1].rearrange("p b t -> p t b"), axis=mybir.AxisListType.X, op=ALU.add
+                    )
+                    part_sq = work.tile([P, B_TILES], F32, name="part_sq")
+                    nc.vector.tensor_reduce(
+                        out=part_sq[:], in_=sq_sums[:, 0 : BLOCKS - 1].rearrange("p b t -> p t b"), axis=mybir.AxisListType.X, op=ALU.add
+                    )
+                    part_neg_mean = work.tile([P, B_TILES], F32, name="part_neg_mean")
+                    nc.vector.tensor_scalar_mul(out=part_neg_mean[:], in0=part_sum[:], scalar1=-1.0 / H)
+                    part_var = work.tile([P, B_TILES], F32, name="part_var")
+                    nc.vector.tensor_scalar(
+                        out=part_var[:], in0=part_sq[:], scalar1=1.0 / H, scalar2=EPS, op0=ALU.mult, op1=ALU.add
+                    )
 
-            blend_sum = work.tile([P, B_TILES], F32, name="blend_sum", tag="blend_sum")
-            nc.vector.tensor_reduce(out=blend_sum[:], in_=blend_sums[:], axis=mybir.AxisListType.X, op=ALU.add)
-            layer_norm(blend, blend_sum[:], H, GAMMA_H_AT, BETA_H_AT, new_h, store_and_turn_new_h)
-
-            out_acc = [psum_acc.tile([P, D], F32, name="out_acc%d" % t, tag="acc") for t in range(B_TILES)]
-            second_matmul(out_acc)
-            pre_out_sum = work.tile([P, B_TILES], F32, name="pre_out_sum", tag="pre_out_sum")
-            for t in range(B_TILES):
-                nc.vector.scalar_tensor_tensor(
-                    out=pre_out[:, t, :], in0=out_acc[t][:], scalar=1.0, in1=bd_all[:],
-                    op0=ALU.mult, op1=ALU.add, accum_out=pre_out_sum[:, t : t + 1],
-                )
-            layer_norm(pre_out, pre_out_sum[:], D, GAMMA_O_AT, BETA_O_AT, out_sb, store_out)
+            last = BLOCKS - 1
+            square_sums(last)
+            nc.vector.scalar_tensor_tensor(
+                out=neg_mean[:], in0=blend_sums[:, last, :], scalar=-1.0 / H, in1=part_neg_mean[:], op0=ALU.mult, op1=ALU.add
+            )
+            off = work.tile([P, B_TILES], F32, name="off")
+            off_sq = work.tile([P, B_TILES], F32, name="off_sq")
+            var_rest = work.tile([P, B_TILES], F32, name="var_rest")
+            var_eps = work.tile([P, B_TILES], F32, name="var_eps")
+            nc.gpsimd.tensor_tensor(out=off[:], in0=neg_mean[:], in1=neg_centre[:], op=ALU.subtract)
+            nc.gpsimd.tensor_tensor(out=off_sq[:], in0=off[:], in1=off[:], op=ALU.mult)
+            nc.gpsimd.tensor_tensor(out=var_rest[:], in0=part_var[:], in1=off_sq[:], op=ALU.subtract)
+            apply_gain(0, 0)
+            nc.vector.scalar_tensor_tensor(
+                out=var_eps[:], in0=sq_sums[:, last, :], scalar=1.0 / H, in1=var_rest[:], op0=ALU.mult, op1=ALU.add
+            )
+            nc.gpsimd.tensor_tensor(out=rstd[:], in0=var_eps[:], in1=neg_half[:], op=ALU.pow)
+            apply_gain(0, 1)
+            regroup_chunk(WU_CHUNKS + 2, on_scalar=True)
+            for g in range(D_PASSES):
+                apply_shift(0, g)
+            regroup_chunk(WU_CHUNKS + 3, on_scalar=True)
+            apply_gain(1, 0)
+            quantise_chunk(WU_CHUNKS + 1)
+            apply_gain(1, 1)
+            quantise_chunk(WU_CHUNKS + 2)
+            apply_shift(1, 0)
+            quantise_new_h(0, 0, D_PASSES)
+            apply_shift(1, 1)
+            apply_shift(1, 2)
+            quantise_chunk(WU_CHUNKS + 3)
+            second_matmul(0, 0, D_PASSES)
+            apply_shift(1, 3)
+            quantise_new_h(1, 0, 2)
+            second_matmul(1, 0, 2)
+            output_sums(0)
+            quantise_new_h(1, 2, 3)
+            second_matmul(1, 2, 3)
+            quantise_new_h(1, 3, 4)
+            second_matmul(1, 3, 4)
+            output_shift(0)
+            output_sums(1)
+            output_shift(1)

@@ -111,8 +111,8 @@ def tile_recurrentffn_pb_kernel(
             )
 
         x_sb = const.tile([P, B_TILES, D], BF16, name="x_sb")
-        h_sb = const.tile([P, B_TILES, H], BF16, name="h_sb")
-        s_sb = const.tile([P, B_TILES, H], BF16, name="s_sb")
+        h_blocks = [const.tile([P, B_TILES, BANK], BF16, name="h_block%d" % b) for b in range(BLOCKS)]
+        s_blocks = [const.tile([P, B_TILES, BANK], BF16, name="s_block%d" % b) for b in range(BLOCKS)]
         comb_grouped = const.tile([P, U_PASSES, B, PACK], BF16, name="comb_grouped", align_bytes=64)
         comb_codes = const.tile([P, U_PASSES, B], U32, name="comb_codes", align_bytes=64)
         comb_scales = const.tile([P, U_PASSES, B], U8, name="comb_scales", align_bytes=64)
@@ -120,7 +120,7 @@ def tile_recurrentffn_pb_kernel(
         def turn_activations(g):
             turned = psum_turn.tile([P, 2, B], F32, name="turned", tag="turn")
             for t in range(B_TILES):
-                feats = x_sb[:, t, :] if g == 0 else h_sb[:, t, (g - 1) * K_PASS : g * K_PASS]
+                feats = x_sb[:, t, :] if g == 0 else h_blocks[g - 1][:, t, :]
                 words = feats.bitcast(F32).rearrange("r (q u) -> r u q", u=2)
                 for u in range(2):
                     nc.tensor.transpose(turned[:, u, t * P : (t + 1) * P], words[:, u, :], ident[:])
@@ -146,14 +146,14 @@ def tile_recurrentffn_pb_kernel(
             diff = psum_diff.tile([P, 2, B], F32, name="diff", tag="diff")
             diffs[block, pair] = diff
             for half in range(2):
-                first = block * BANK + (2 * pair + half) * P
+                feats = slice((2 * pair + half) * P, (2 * pair + half + 1) * P)
                 for t in range(B_TILES):
                     rows = slice(t * P, (t + 1) * P)
                     nc.tensor.matmul(
-                        out=diff[:, half, rows], lhsT=s_sb[:, t, first : first + P], rhs=plus_ident[:], start=True, stop=False
+                        out=diff[:, half, rows], lhsT=s_blocks[block][:, t, feats], rhs=plus_ident[:], start=True, stop=False
                     )
                     nc.tensor.matmul(
-                        out=diff[:, half, rows], lhsT=h_sb[:, t, first : first + P], rhs=minus_ident[:], start=False, stop=True
+                        out=diff[:, half, rows], lhsT=h_blocks[block][:, t, feats], rhs=minus_ident[:], start=False, stop=True
                     )
 
         def first_matmul(i):
@@ -201,7 +201,7 @@ def tile_recurrentffn_pb_kernel(
             cols = slice(block * BANK, (block + 1) * BANK)
             for t in range(B_TILES):
                 nc.vector.scalar_tensor_tensor(
-                    out=blend[:, t, cols], in0=h_sb[:, t, cols], scalar=2.0, in1=product_banks[block, t][:],
+                    out=blend[:, t, cols], in0=h_blocks[block][:, t, :], scalar=2.0, in1=product_banks[block, t][:],
                     op0=ALU.mult, op1=ALU.add, accum_out=blend_sums[:, block, t : t + 1],
                 )
             if block == 0:
@@ -270,10 +270,10 @@ def tile_recurrentffn_pb_kernel(
 
         pre_out = const.tile([P, B_TILES, D], F32, name="pre_out")
         out_sb = const.tile([P, B_TILES, D], F32, name="out_sb")
-        out_stats = [[work.tile([P, 1], F32, name="out_%s%d" % (what, t)) for what in ("sum", "mean", "sq", "var", "rstd")] for t in range(B_TILES)]
+        out_stats = [[work.tile([P, 1], F32, name="out_%s%d" % (what, t)) for what in ("sum", "mean", "sq", "rstd")] for t in range(B_TILES)]
 
         def output_sums(t):
-            total, neg, sq, var, rs = out_stats[t]
+            total, neg, sq, rs = out_stats[t]
             nc.vector.scalar_tensor_tensor(
                 out=pre_out[:, t, :], in0=out_acc[t][:], scalar=1.0, in1=b_d_all[:],
                 op0=ALU.mult, op1=ALU.add, accum_out=total[:],
@@ -283,96 +283,107 @@ def tile_recurrentffn_pb_kernel(
             nc.scalar.activation(
                 out=squares[:], in_=pre_out[:, t, :], func=ACT.Square, bias=neg[:], scale=1.0, accum_out=sq[:]
             )
-            nc.gpsimd.tensor_scalar(out=var[:], in0=sq[:], scalar1=1.0 / D, scalar2=EPS, op0=ALU.mult, op1=ALU.add)
-            nc.gpsimd.tensor_tensor(out=rs[:], in0=var[:], in1=neg_half[:, 0:1], op=ALU.pow)
+            nc.scalar.activation(out=rs[:], in_=sq[:], func=ACT.Abs_reciprocal_sqrt, bias=EPS, scale=1.0 / D)
             nc.vector.scalar_tensor_tensor(
                 out=out_sb[:, t, :], in0=pre_out[:, t, :], scalar=neg[:], in1=gamma_o_all[:], op0=ALU.add, op1=ALU.mult
             )
 
         def output_shift(t):
             nc.vector.scalar_tensor_tensor(
-                out=out_sb[:, t, :], in0=out_sb[:, t, :], scalar=out_stats[t][4][:], in1=beta_o_all[:],
+                out=out_sb[:, t, :], in0=out_sb[:, t, :], scalar=out_stats[t][3][:], in1=beta_o_all[:],
                 op0=ALU.mult, op1=ALU.add,
             )
             nc.sync.dma_start(out=out_0[t * P : (t + 1) * P, :], in_=out_sb[:, t, :])
 
         with tc.manual_schedule():
             by_tile = lambda dram: dram.rearrange("(t r) k -> r t k", r=P)
+            H_LOADED_BEHIND = (1, 3, 4, 5)
             for i in range(CHUNKS):
                 load_chunk(i)
                 if i == 1:
                     nc.sync.dma_start(out=x_sb[:], in_=by_tile(x))
-                if 1 <= i <= BLOCKS:
-                    cols = slice((i - 1) * BANK, i * BANK)
-                    nc.sync.dma_start(out=h_sb[:, :, cols], in_=by_tile(hidden_state)[:, :, cols])
+                if i in H_LOADED_BEHIND:
+                    b = H_LOADED_BEHIND.index(i)
+                    cols = slice(b * BANK, (b + 1) * BANK)
+                    nc.sync.dma_start(out=h_blocks[b][:], in_=by_tile(hidden_state)[:, :, cols])
                 if i == 2:
                     nc.sync.dma_start(out=bu_rows[0:BU_COLS, :], in_=b_u.rearrange("(c q) -> c q", q=P))
                 if i < WU_CHUNKS and i % U_PASSES == U_PASSES - 1:
                     cols = slice(i // U_PASSES * BANK, (i // U_PASSES + 1) * BANK)
-                    nc.sync.dma_start(out=s_sb[:, :, cols], in_=by_tile(swiglu)[:, :, cols])
+                    nc.sync.dma_start(out=s_blocks[i // U_PASSES][:], in_=by_tile(swiglu)[:, :, cols])
             for vec, tile in (
                 (gamma_h, gamma_h_all), (beta_h, beta_h_all), (b_d, b_d_all), (gamma_o, gamma_o_all), (beta_o, beta_o_all)
             ):
                 nc.sync.dma_start(out=tile[:], in_=vec.partition_broadcast(P))
 
-            FIRST_END = U_PASSES - 1 + QUANTISE_LAG
-            last_round = FIRST_END + BLOCKS * U_PASSES
-            for i in range(last_round + 1):
-                block, since = divmod(i - FIRST_END, U_PASSES)
-                live = 0 <= block < BLOCKS
-                if live and since in (1, 2):
-                    sigmoid(block, since - 1)
-                if live and since in (3, 4):
-                    turn_product(block, since - 3)
-                if since == 2 and 1 <= block < BLOCKS:
-                    square_sums(block - 1)
+            TURN_ROUND = (1, 2, 4, 5, 6)
+            LAST_PASS = [TURN_ROUND[-1] + 1] + [(b + 1) * U_PASSES - 1 + QUANTISE_LAG for b in range(1, BLOCKS)]
+
+            def pass_round(i):
+                block, g = divmod(i, U_PASSES)
+                if block == 0:
+                    return TURN_ROUND[g] + 1
+                return max(i + QUANTISE_LAG, LAST_PASS[block - 1] + 2)
+
+            for i in range(LAST_PASS[-1] + 6):
+                since = [i - last for last in LAST_PASS]
+                for b in range(BLOCKS):
+                    if since[b] in (1, 2):
+                        sigmoid(b, since[b] - 1)
+                    if since[b] in (3, 4):
+                        turn_product(b, since[b] - 3)
+                    if since[b] == -1:
+                        turn_difference(b, 0)
+                for b in range(BLOCKS - 1):
+                    if since[b] == 7:
+                        square_sums(b)
                 if i < WU_CHUNKS:
                     regroup_chunk(i, on_scalar=(i % 2 == 0))
                 if i == WU_CHUNKS:
                     regroup_chunk(WU_CHUNKS, on_scalar=True)
                 if 0 <= i - QUANTISE_LAG < WU_CHUNKS:
                     quantise_chunk(i - QUANTISE_LAG)
-                if i == WU_CHUNKS + 2:
-                    regroup_chunk(WU_CHUNKS + 1, on_scalar=False)
-                if 1 <= i <= U_PASSES:
-                    turn_activations(i - 1)
-                if 2 <= i <= U_PASSES + 1:
-                    quantise_activations(i - 2)
+                for g in range(U_PASSES):
+                    if i == TURN_ROUND[g]:
+                        turn_activations(g)
+                    if i == TURN_ROUND[g] + 1:
+                        quantise_activations(g)
                 if i == U_PASSES:
                     bu_turned = turn_b_u()
                 if i == U_PASSES + 1:
                     nc.vector.tensor_copy(out=bu_cols[:], in_=bu_turned[:, 0:BU_COLS])
-                if i == last_round:
-                    quantise_chunk(WU_CHUNKS)
-                if since == 0 and 1 <= block <= BLOCKS:
-                    add_hidden(block - 1)
-                if live and since in (2, 3):
-                    gate_difference(block, since - 2)
-                if 0 <= i - QUANTISE_LAG < WU_CHUNKS:
-                    first_matmul(i - QUANTISE_LAG)
-                ahead, left = divmod(i - FIRST_END + 2, U_PASSES)
-                if 0 <= ahead < BLOCKS and left < PAIRS:
-                    turn_difference(ahead, left)
-                if i == last_round - 1:
+                for b in range(BLOCKS):
+                    if since[b] == 5:
+                        add_hidden(b)
+                    if since[b] in (2, 3):
+                        gate_difference(b, since[b] - 2)
+                for chunk in range(WU_CHUNKS):
+                    if i == pass_round(chunk):
+                        first_matmul(chunk)
+                for b in range(BLOCKS):
+                    if since[b] == 0:
+                        turn_difference(b, 1)
+                if i == LAST_PASS[-1] + 4:
                     part_sum = work.tile([P, B_TILES], F32, name="part_sum")
                     nc.vector.tensor_reduce(
                         out=part_sum[:], in_=blend_sums[:, 0 : BLOCKS - 1].rearrange("p b t -> p t b"), axis=mybir.AxisListType.X, op=ALU.add
                     )
-                    part_sq = work.tile([P, B_TILES], F32, name="part_sq")
-                    nc.vector.tensor_reduce(
-                        out=part_sq[:], in_=sq_sums[:, 0 : BLOCKS - 1].rearrange("p b t -> p t b"), axis=mybir.AxisListType.X, op=ALU.add
-                    )
                     part_neg_mean = work.tile([P, B_TILES], F32, name="part_neg_mean")
                     nc.vector.tensor_scalar_mul(out=part_neg_mean[:], in0=part_sum[:], scalar1=-1.0 / H)
-                    part_var = work.tile([P, B_TILES], F32, name="part_var")
-                    nc.vector.tensor_scalar(
-                        out=part_var[:], in0=part_sq[:], scalar1=1.0 / H, scalar2=EPS, op0=ALU.mult, op1=ALU.add
-                    )
 
             last = BLOCKS - 1
+            nc.scalar.activation(out=warm[:], in_=neg_half[:, 0:1], func=ACT.Abs_reciprocal_sqrt)
             square_sums(last)
             nc.vector.scalar_tensor_tensor(
                 out=neg_mean[:], in0=blend_sums[:, last, :], scalar=-1.0 / H, in1=part_neg_mean[:], op0=ALU.mult, op1=ALU.add
+            )
+            part_sq = work.tile([P, B_TILES], F32, name="part_sq")
+            nc.vector.tensor_reduce(
+                out=part_sq[:], in_=sq_sums[:, 0:last].rearrange("p b t -> p t b"), axis=mybir.AxisListType.X, op=ALU.add
+            )
+            part_var = work.tile([P, B_TILES], F32, name="part_var")
+            nc.gpsimd.tensor_scalar(
+                out=part_var[:], in0=part_sq[:], scalar1=1.0 / H, scalar2=EPS, op0=ALU.mult, op1=ALU.add
             )
             off = work.tile([P, B_TILES], F32, name="off")
             off_sq = work.tile([P, B_TILES], F32, name="off_sq")
@@ -387,28 +398,26 @@ def tile_recurrentffn_pb_kernel(
             )
             nc.gpsimd.tensor_tensor(out=rstd[:], in0=var_eps[:], in1=neg_half[:], op=ALU.pow)
             apply_gain(0, 1)
-            regroup_chunk(WU_CHUNKS + 2, on_scalar=True)
+            regroup_chunk(WU_CHUNKS + 1, on_scalar=True)
             for g in range(D_PASSES):
                 apply_shift(0, g)
+            regroup_chunk(WU_CHUNKS + 2, on_scalar=True)
             regroup_chunk(WU_CHUNKS + 3, on_scalar=True)
             apply_gain(1, 0)
-            quantise_chunk(WU_CHUNKS + 1)
+            quantise_chunk(WU_CHUNKS)
             apply_gain(1, 1)
-            quantise_chunk(WU_CHUNKS + 2)
+            quantise_chunk(WU_CHUNKS + 1)
             apply_shift(1, 0)
             quantise_new_h(0, 0, D_PASSES)
-            apply_shift(1, 1)
-            apply_shift(1, 2)
+            for g in range(1, D_PASSES):
+                apply_shift(1, g)
+            quantise_chunk(WU_CHUNKS + 2)
             quantise_chunk(WU_CHUNKS + 3)
             second_matmul(0, 0, D_PASSES)
-            apply_shift(1, 3)
             quantise_new_h(1, 0, 2)
-            second_matmul(1, 0, 2)
             output_sums(0)
-            quantise_new_h(1, 2, 3)
-            second_matmul(1, 2, 3)
-            quantise_new_h(1, 3, 4)
-            second_matmul(1, 3, 4)
+            quantise_new_h(1, 2, 4)
+            second_matmul(1, 0, D_PASSES)
             output_shift(0)
             output_sums(1)
             output_shift(1)

@@ -28,6 +28,9 @@ PAIRS = H_TILES // 2
 WU_CHUNKS = BLOCKS * U_PASSES
 CHUNKS = WU_CHUNKS + D_PASSES
 BU_COLS = H // P
+GAMMA_H_AT, BETA_H_AT = 0, H // P
+B_D_AT, GAMMA_O_AT, BETA_O_AT = 2 * H // P, 2 * H // P + D // P, 2 * H // P + 2 * D // P
+REST_COLS = 2 * H // P + 3 * D // P
 
 RUN = 4
 QUANTISE_LAG = 2
@@ -63,16 +66,23 @@ def tile_recurrentffn_pb_kernel(
         bu_rows = const.tile([P, P], BF16, name="bu_rows")
         nc.vector.memset(bu_rows[:], 0.0)
         bu_cols = const.tile([P, BU_COLS], F32, name="bu_cols")
-        gamma_h_all = const.tile([P, H], BF16, name="gamma_h_all")
-        beta_h_all = const.tile([P, H], BF16, name="beta_h_all")
-        b_d_all = const.tile([P, D], BF16, name="b_d_all")
-        gamma_o_all = const.tile([P, D], BF16, name="gamma_o_all")
-        beta_o_all = const.tile([P, D], BF16, name="beta_o_all")
+        rest_rows = const.tile([P, P], BF16, name="rest_rows")
+        nc.vector.memset(rest_rows[:], 0.0)
+        rest_cols = const.tile([P, REST_COLS], F32, name="rest_cols")
+        b_d_all = const.tile([P, D], F32, name="b_d_all")
 
-        def turn_b_u():
-            turned = psum_turn.tile([P, P], BF16, name="bu_turned", tag="turn")
-            nc.tensor.transpose(turned[:], bu_rows[:], plus_ident[:])
+        def turn_rows(rows):
+            turned = psum_turn.tile([P, P], BF16, name="rows_turned", tag="turn")
+            nc.tensor.transpose(turned[:], rows[:], plus_ident[:])
             return turned
+
+        def spread(at, pool, tag):
+            bank = pool.tile([P, BANK], F32, name="spread_bank", tag=tag)
+            for c in range(BANK // P):
+                nc.tensor.transpose(
+                    bank[:, c * P : (c + 1) * P], rest_cols[:, at + c : at + c + 1].to_broadcast([P, P]), ident[:]
+                )
+            return bank
 
         wu_codes = const.tile([P, WU_CHUNKS, BANK], U32, name="wu_codes", align_bytes=64)
         wu_scales = const.tile([P, WU_CHUNKS, BANK], U8, name="wu_scales", align_bytes=64)
@@ -222,19 +232,18 @@ def tile_recurrentffn_pb_kernel(
         nh_scales = const.tile([P, B_TILES, D_PASSES, P], U8, name="nh_scales", align_bytes=64)
         neg_mean = const.tile([P, B_TILES], F32, name="neg_mean")
         rstd = const.tile([P, B_TILES], F32, name="rstd")
-        GAIN_COLS = 2 * BANK
 
-        def apply_gain(t, piece):
-            cols = slice(piece * GAIN_COLS, (piece + 1) * GAIN_COLS)
+        def apply_gain(t, g, gain):
+            cols = slice(g * K_PASS, (g + 1) * K_PASS)
             nc.vector.scalar_tensor_tensor(
-                out=new_h[:, t, cols], in0=blend[:, t, cols], scalar=neg_mean[:, t : t + 1], in1=gamma_h_all[:, cols],
+                out=new_h[:, t, cols], in0=blend[:, t, cols], scalar=neg_mean[:, t : t + 1], in1=gain[:],
                 op0=ALU.add, op1=ALU.mult,
             )
 
-        def apply_shift(t, g):
+        def apply_shift(t, g, shift):
             cols = slice(g * K_PASS, (g + 1) * K_PASS)
             nc.vector.scalar_tensor_tensor(
-                out=new_h[:, t, cols], in0=new_h[:, t, cols], scalar=rstd[:, t : t + 1], in1=beta_h_all[:, cols],
+                out=new_h[:, t, cols], in0=new_h[:, t, cols], scalar=rstd[:, t : t + 1], in1=shift[:],
                 op0=ALU.mult, op1=ALU.add,
             )
             nc.sync.dma_start(out=out_1[t * P : (t + 1) * P, cols], in_=new_h[:, t, cols])
@@ -272,7 +281,7 @@ def tile_recurrentffn_pb_kernel(
         out_sb = const.tile([P, B_TILES, D], F32, name="out_sb")
         out_stats = [[work.tile([P, 1], F32, name="out_%s%d" % (what, t)) for what in ("sum", "mean", "sq", "rstd")] for t in range(B_TILES)]
 
-        def output_sums(t):
+        def output_sums(t, gain):
             total, neg, sq, rs = out_stats[t]
             nc.vector.scalar_tensor_tensor(
                 out=pre_out[:, t, :], in0=out_acc[t][:], scalar=1.0, in1=b_d_all[:],
@@ -285,18 +294,19 @@ def tile_recurrentffn_pb_kernel(
             )
             nc.scalar.activation(out=rs[:], in_=sq[:], func=ACT.Abs_reciprocal_sqrt, bias=EPS, scale=1.0 / D)
             nc.vector.scalar_tensor_tensor(
-                out=out_sb[:, t, :], in0=pre_out[:, t, :], scalar=neg[:], in1=gamma_o_all[:], op0=ALU.add, op1=ALU.mult
+                out=out_sb[:, t, :], in0=pre_out[:, t, :], scalar=neg[:], in1=gain[:], op0=ALU.add, op1=ALU.mult
             )
 
-        def output_shift(t):
+        def output_shift(t, shift):
             nc.vector.scalar_tensor_tensor(
-                out=out_sb[:, t, :], in0=out_sb[:, t, :], scalar=out_stats[t][3][:], in1=beta_o_all[:],
+                out=out_sb[:, t, :], in0=out_sb[:, t, :], scalar=out_stats[t][3][:], in1=shift[:],
                 op0=ALU.mult, op1=ALU.add,
             )
             nc.sync.dma_start(out=out_0[t * P : (t + 1) * P, :], in_=out_sb[:, t, :])
 
         with tc.manual_schedule():
             by_tile = lambda dram: dram.rearrange("(t r) k -> r t k", r=P)
+            rest_vectors = ((gamma_h, GAMMA_H_AT), (beta_h, BETA_H_AT), (b_d, B_D_AT), (gamma_o, GAMMA_O_AT), (beta_o, BETA_O_AT))
             H_LOADED_BEHIND = (1, 3, 4, 5)
             for i in range(CHUNKS):
                 load_chunk(i)
@@ -306,15 +316,14 @@ def tile_recurrentffn_pb_kernel(
                     b = H_LOADED_BEHIND.index(i)
                     cols = slice(b * BANK, (b + 1) * BANK)
                     nc.sync.dma_start(out=h_blocks[b][:], in_=by_tile(hidden_state)[:, :, cols])
+                if U_PASSES < i <= U_PASSES + len(rest_vectors):
+                    vec, at = rest_vectors[i - U_PASSES - 1]
+                    nc.sync.dma_start(out=rest_rows[at : at + vec.shape[0] // P, :], in_=vec.rearrange("(c q) -> c q", q=P))
                 if i == 2:
                     nc.sync.dma_start(out=bu_rows[0:BU_COLS, :], in_=b_u.rearrange("(c q) -> c q", q=P))
                 if i < WU_CHUNKS and i % U_PASSES == U_PASSES - 1:
                     cols = slice(i // U_PASSES * BANK, (i // U_PASSES + 1) * BANK)
                     nc.sync.dma_start(out=s_blocks[i // U_PASSES][:], in_=by_tile(swiglu)[:, :, cols])
-            for vec, tile in (
-                (gamma_h, gamma_h_all), (beta_h, beta_h_all), (b_d, b_d_all), (gamma_o, gamma_o_all), (beta_o, beta_o_all)
-            ):
-                nc.sync.dma_start(out=tile[:], in_=vec.partition_broadcast(P))
 
             TURN_ROUND = (1, 2, 4, 5, 6)
             LAST_PASS = [TURN_ROUND[-1] + 1] + [(b + 1) * U_PASSES - 1 + QUANTISE_LAG for b in range(1, BLOCKS)]
@@ -349,9 +358,13 @@ def tile_recurrentffn_pb_kernel(
                     if i == TURN_ROUND[g] + 1:
                         quantise_activations(g)
                 if i == U_PASSES:
-                    bu_turned = turn_b_u()
+                    bu_turned = turn_rows(bu_rows)
                 if i == U_PASSES + 1:
                     nc.vector.tensor_copy(out=bu_cols[:], in_=bu_turned[:, 0:BU_COLS])
+                if i == LAST_PASS[1] + 5:
+                    rest_turned = turn_rows(rest_rows)
+                if i == LAST_PASS[1] + 6:
+                    nc.vector.tensor_copy(out=rest_cols[:], in_=rest_turned[:, 0:REST_COLS])
                 for b in range(BLOCKS):
                     if since[b] == 5:
                         add_hidden(b)
@@ -392,32 +405,40 @@ def tile_recurrentffn_pb_kernel(
             nc.gpsimd.tensor_tensor(out=off[:], in0=neg_mean[:], in1=neg_centre[:], op=ALU.subtract)
             nc.gpsimd.tensor_tensor(out=off_sq[:], in0=off[:], in1=off[:], op=ALU.mult)
             nc.gpsimd.tensor_tensor(out=var_rest[:], in0=part_var[:], in1=off_sq[:], op=ALU.subtract)
-            apply_gain(0, 0)
-            nc.vector.scalar_tensor_tensor(
-                out=var_eps[:], in0=sq_sums[:, last, :], scalar=1.0 / H, in1=var_rest[:], op0=ALU.mult, op1=ALU.add
-            )
-            nc.gpsimd.tensor_tensor(out=rstd[:], in0=var_eps[:], in1=neg_half[:], op=ALU.pow)
-            apply_gain(0, 1)
+            gain = [spread(GAMMA_H_AT + g * H_TILES, psum_diff, "diff") for g in range(2)]
+            shift = [spread(BETA_H_AT + g * H_TILES, psum_acc, "acc") for g in range(D_PASSES)]
             regroup_chunk(WU_CHUNKS + 1, on_scalar=True)
             for g in range(D_PASSES):
-                apply_shift(0, g)
+                for t in range(B_TILES):
+                    apply_gain(t, g, gain[g])
+                if g + 2 < D_PASSES:
+                    gain.append(spread(GAMMA_H_AT + (g + 2) * H_TILES, psum_diff, "diff"))
+                if g == 1:
+                    nc.vector.scalar_tensor_tensor(
+                        out=var_eps[:], in0=sq_sums[:, last, :], scalar=1.0 / H, in1=var_rest[:], op0=ALU.mult, op1=ALU.add
+                    )
+                    nc.gpsimd.tensor_tensor(out=rstd[:], in0=var_eps[:], in1=neg_half[:], op=ALU.pow)
             regroup_chunk(WU_CHUNKS + 2, on_scalar=True)
-            regroup_chunk(WU_CHUNKS + 3, on_scalar=True)
-            apply_gain(1, 0)
+            b_d_bank = spread(B_D_AT, psum_turn, "turn")
+            nc.scalar.copy(out=b_d_all[:], in_=b_d_bank[:])
             quantise_chunk(WU_CHUNKS)
-            apply_gain(1, 1)
+            for g in range(D_PASSES):
+                apply_shift(0, g, shift[g])
+            regroup_chunk(WU_CHUNKS + 3, on_scalar=True)
             quantise_chunk(WU_CHUNKS + 1)
-            apply_shift(1, 0)
+            apply_shift(1, 0, shift[0])
             quantise_new_h(0, 0, D_PASSES)
-            for g in range(1, D_PASSES):
-                apply_shift(1, g)
             quantise_chunk(WU_CHUNKS + 2)
+            for g in range(1, D_PASSES):
+                apply_shift(1, g, shift[g])
             quantise_chunk(WU_CHUNKS + 3)
             second_matmul(0, 0, D_PASSES)
+            out_gain = spread(GAMMA_O_AT, psum_acc, "acc")
+            out_shift = spread(BETA_O_AT, psum_acc, "acc")
             quantise_new_h(1, 0, 2)
-            output_sums(0)
             quantise_new_h(1, 2, 4)
             second_matmul(1, 0, D_PASSES)
-            output_shift(0)
-            output_sums(1)
-            output_shift(1)
+            output_sums(0, out_gain)
+            output_sums(1, out_gain)
+            output_shift(0, out_shift)
+            output_shift(1, out_shift)

@@ -347,7 +347,7 @@ def tile_recurrentffn_pb_kernel(
                     if since[b] == 7:
                         square_sums(b)
                 if i < WU_CHUNKS:
-                    regroup_chunk(i, on_scalar=(i % 2 == 0))
+                    regroup_chunk(i, on_scalar=(i % U_PASSES in (0, 2)))
                 if i == WU_CHUNKS:
                     regroup_chunk(WU_CHUNKS, on_scalar=True)
                 if 0 <= i - QUANTISE_LAG < WU_CHUNKS:

@@ -32,7 +32,7 @@ GAMMA_H_AT, BETA_H_AT = 0, H // P
 B_D_AT, GAMMA_O_AT, BETA_O_AT = 2 * H // P, 2 * H // P + D // P, 2 * H // P + 2 * D // P
 REST_COLS = 2 * H // P + 3 * D // P
 
-RUN = 4
+RUN = 8
 QUANTISE_LAG = 2
 
 FLOPS = 2 * B * C * H + 2 * B * H * D

@@ -70,6 +70,8 @@ def tile_recurrentffn_pb_kernel(
         nc.vector.memset(rest_rows[:], 0.0)
         rest_cols = const.tile([P, REST_COLS], F32, name="rest_cols")
         b_d_all = const.tile([P, D], F32, name="b_d_all")
+        last_gain = const.tile([P, BANK], BF16, name="last_gain")
+        last_shift = const.tile([P, BANK], BF16, name="last_shift")
 
         def turn_rows(rows):
             turned = psum_turn.tile([P, P], BF16, name="rows_turned", tag="turn")
@@ -240,12 +242,24 @@ def tile_recurrentffn_pb_kernel(
                 op0=ALU.add, op1=ALU.mult,
             )
 
+        def normalise_on_gpsimd(t, g):
+            cols = slice(g * K_PASS, (g + 1) * K_PASS)
+            nc.gpsimd.tensor_scalar(
+                out=new_h[:, t, cols], in0=blend[:, t, cols], scalar1=neg_mean[:, t : t + 1], scalar2=rstd[:, t : t + 1],
+                op0=ALU.add, op1=ALU.mult,
+            )
+            nc.gpsimd.tensor_tensor(out=new_h[:, t, cols], in0=new_h[:, t, cols], in1=last_gain[:], op=ALU.mult)
+            nc.gpsimd.tensor_tensor(out=new_h[:, t, cols], in0=new_h[:, t, cols], in1=last_shift[:], op=ALU.add)
+
         def apply_shift(t, g, shift):
             cols = slice(g * K_PASS, (g + 1) * K_PASS)
             nc.vector.scalar_tensor_tensor(
                 out=new_h[:, t, cols], in0=new_h[:, t, cols], scalar=rstd[:, t : t + 1], in1=shift[:],
                 op0=ALU.mult, op1=ALU.add,
             )
+
+        def store_and_turn(t, g):
+            cols = slice(g * K_PASS, (g + 1) * K_PASS)
             nc.sync.dma_start(out=out_1[t * P : (t + 1) * P, cols], in_=new_h[:, t, cols])
             pool, tag = (psum_turn, "turn") if g % 2 == 0 else (psum_diff, "diff")
             turned = pool.tile([P, PACK, P], F32, name="nh_turned", tag=tag)
@@ -316,8 +330,8 @@ def tile_recurrentffn_pb_kernel(
                     b = H_LOADED_BEHIND.index(i)
                     cols = slice(b * BANK, (b + 1) * BANK)
                     nc.sync.dma_start(out=h_blocks[b][:], in_=by_tile(hidden_state)[:, :, cols])
-                if U_PASSES < i <= U_PASSES + len(rest_vectors):
-                    vec, at = rest_vectors[i - U_PASSES - 1]
+                if 2 < i <= 2 + len(rest_vectors):
+                    vec, at = rest_vectors[i - 3]
                     nc.sync.dma_start(out=rest_rows[at : at + vec.shape[0] // P, :], in_=vec.rearrange("(c q) -> c q", q=P))
                 if i == 2:
                     nc.sync.dma_start(out=bu_rows[0:BU_COLS, :], in_=b_u.rearrange("(c q) -> c q", q=P))
@@ -325,17 +339,22 @@ def tile_recurrentffn_pb_kernel(
                     cols = slice(i // U_PASSES * BANK, (i // U_PASSES + 1) * BANK)
                     nc.sync.dma_start(out=s_blocks[i // U_PASSES][:], in_=by_tile(swiglu)[:, :, cols])
 
+            for vec, tile in ((gamma_h, last_gain), (beta_h, last_shift)):
+                nc.sync.dma_start(out=tile[:], in_=vec[H - BANK : H].partition_broadcast(P))
+
             TURN_ROUND = (1, 2, 4, 5, 6)
             LAST_PASS = [TURN_ROUND[-1] + 1] + [(b + 1) * U_PASSES - 1 + QUANTISE_LAG for b in range(1, BLOCKS)]
+
+            SLACK = [1] * (BLOCKS - 1) + [0]
 
             def pass_round(i):
                 block, g = divmod(i, U_PASSES)
                 if block == 0:
                     return TURN_ROUND[g] + 1
-                return max(i + QUANTISE_LAG, LAST_PASS[block - 1] + 2)
+                return max(i + QUANTISE_LAG, LAST_PASS[block - 1] + SLACK[block - 1] + 2)
 
             for i in range(LAST_PASS[-1] + 6):
-                since = [i - last for last in LAST_PASS]
+                since = [i - last - slack for last, slack in zip(LAST_PASS, SLACK)]
                 for b in range(BLOCKS):
                     if since[b] in (1, 2):
                         sigmoid(b, since[b] - 1)
@@ -347,7 +366,7 @@ def tile_recurrentffn_pb_kernel(
                     if since[b] == 7:
                         square_sums(b)
                 if i < WU_CHUNKS:
-                    regroup_chunk(i, on_scalar=(i % U_PASSES in (0, 2)))
+                    regroup_chunk(i, on_scalar=(i % U_PASSES in (1, 3)))
                 if i == WU_CHUNKS:
                     regroup_chunk(WU_CHUNKS, on_scalar=True)
                 if 0 <= i - QUANTISE_LAG < WU_CHUNKS:
@@ -361,9 +380,9 @@ def tile_recurrentffn_pb_kernel(
                     bu_turned = turn_rows(bu_rows)
                 if i == U_PASSES + 1:
                     nc.vector.tensor_copy(out=bu_cols[:], in_=bu_turned[:, 0:BU_COLS])
-                if i == LAST_PASS[1] + 5:
+                if i == TURN_ROUND[-1] + 1:
                     rest_turned = turn_rows(rest_rows)
-                if i == LAST_PASS[1] + 6:
+                if i == TURN_ROUND[-1] + 2:
                     nc.vector.tensor_copy(out=rest_cols[:], in_=rest_turned[:, 0:REST_COLS])
                 for b in range(BLOCKS):
                     if since[b] == 5:
@@ -405,39 +424,48 @@ def tile_recurrentffn_pb_kernel(
             nc.gpsimd.tensor_tensor(out=off[:], in0=neg_mean[:], in1=neg_centre[:], op=ALU.subtract)
             nc.gpsimd.tensor_tensor(out=off_sq[:], in0=off[:], in1=off[:], op=ALU.mult)
             nc.gpsimd.tensor_tensor(out=var_rest[:], in0=part_var[:], in1=off_sq[:], op=ALU.subtract)
+            pieces = D_PASSES - 1
             gain = [spread(GAMMA_H_AT + g * H_TILES, psum_diff, "diff") for g in range(2)]
-            shift = [spread(BETA_H_AT + g * H_TILES, psum_acc, "acc") for g in range(D_PASSES)]
+            shift = [spread(BETA_H_AT + g * H_TILES, psum_acc, "acc") for g in range(pieces)]
             regroup_chunk(WU_CHUNKS + 1, on_scalar=True)
-            for g in range(D_PASSES):
+            for g in range(pieces):
                 for t in range(B_TILES):
                     apply_gain(t, g, gain[g])
-                if g + 2 < D_PASSES:
+                if g + 2 < pieces:
                     gain.append(spread(GAMMA_H_AT + (g + 2) * H_TILES, psum_diff, "diff"))
-                if g == 1:
+                if g == 0:
                     nc.vector.scalar_tensor_tensor(
                         out=var_eps[:], in0=sq_sums[:, last, :], scalar=1.0 / H, in1=var_rest[:], op0=ALU.mult, op1=ALU.add
                     )
                     nc.gpsimd.tensor_tensor(out=rstd[:], in0=var_eps[:], in1=neg_half[:], op=ALU.pow)
+                    for t in range(B_TILES):
+                        normalise_on_gpsimd(t, pieces)
             regroup_chunk(WU_CHUNKS + 2, on_scalar=True)
             b_d_bank = spread(B_D_AT, psum_turn, "turn")
             nc.scalar.copy(out=b_d_all[:], in_=b_d_bank[:])
             quantise_chunk(WU_CHUNKS)
-            for g in range(D_PASSES):
+            for g in range(pieces):
                 apply_shift(0, g, shift[g])
+                store_and_turn(0, g)
+            store_and_turn(0, pieces)
             regroup_chunk(WU_CHUNKS + 3, on_scalar=True)
             quantise_chunk(WU_CHUNKS + 1)
             apply_shift(1, 0, shift[0])
+            store_and_turn(1, 0)
             quantise_new_h(0, 0, D_PASSES)
             quantise_chunk(WU_CHUNKS + 2)
-            for g in range(1, D_PASSES):
+            for g in range(1, pieces):
                 apply_shift(1, g, shift[g])
+                store_and_turn(1, g)
+            store_and_turn(1, pieces)
             quantise_chunk(WU_CHUNKS + 3)
             second_matmul(0, 0, D_PASSES)
             out_gain = spread(GAMMA_O_AT, psum_acc, "acc")
             out_shift = spread(BETA_O_AT, psum_acc, "acc")
             quantise_new_h(1, 0, 2)
+            second_matmul(1, 0, 2)
             quantise_new_h(1, 2, 4)
-            second_matmul(1, 0, D_PASSES)
+            second_matmul(1, 2, 4)
             output_sums(0, out_gain)
             output_sums(1, out_gain)
             output_shift(0, out_shift)

@@ -70,8 +70,6 @@ def tile_recurrentffn_pb_kernel(
         nc.vector.memset(rest_rows[:], 0.0)
         rest_cols = const.tile([P, REST_COLS], F32, name="rest_cols")
         b_d_all = const.tile([P, D], F32, name="b_d_all")
-        last_gain = const.tile([P, BANK], BF16, name="last_gain")
-        last_shift = const.tile([P, BANK], BF16, name="last_shift")
 
         def turn_rows(rows):
             turned = psum_turn.tile([P, P], BF16, name="rows_turned", tag="turn")
@@ -242,24 +240,12 @@ def tile_recurrentffn_pb_kernel(
                 op0=ALU.add, op1=ALU.mult,
             )
 
-        def normalise_on_gpsimd(t, g):
-            cols = slice(g * K_PASS, (g + 1) * K_PASS)
-            nc.gpsimd.tensor_scalar(
-                out=new_h[:, t, cols], in0=blend[:, t, cols], scalar1=neg_mean[:, t : t + 1], scalar2=rstd[:, t : t + 1],
-                op0=ALU.add, op1=ALU.mult,
-            )
-            nc.gpsimd.tensor_tensor(out=new_h[:, t, cols], in0=new_h[:, t, cols], in1=last_gain[:], op=ALU.mult)
-            nc.gpsimd.tensor_tensor(out=new_h[:, t, cols], in0=new_h[:, t, cols], in1=last_shift[:], op=ALU.add)
-
         def apply_shift(t, g, shift):
             cols = slice(g * K_PASS, (g + 1) * K_PASS)
             nc.vector.scalar_tensor_tensor(
                 out=new_h[:, t, cols], in0=new_h[:, t, cols], scalar=rstd[:, t : t + 1], in1=shift[:],
                 op0=ALU.mult, op1=ALU.add,
             )
-
-        def store_and_turn(t, g):
-            cols = slice(g * K_PASS, (g + 1) * K_PASS)
             nc.sync.dma_start(out=out_1[t * P : (t + 1) * P, cols], in_=new_h[:, t, cols])
             pool, tag = (psum_turn, "turn") if g % 2 == 0 else (psum_diff, "diff")
             turned = pool.tile([P, PACK, P], F32, name="nh_turned", tag=tag)
@@ -338,9 +324,6 @@ def tile_recurrentffn_pb_kernel(
                 if i < WU_CHUNKS and i % U_PASSES == U_PASSES - 1:
                     cols = slice(i // U_PASSES * BANK, (i // U_PASSES + 1) * BANK)
                     nc.sync.dma_start(out=s_blocks[i // U_PASSES][:], in_=by_tile(swiglu)[:, :, cols])
-
-            for vec, tile in ((gamma_h, last_gain), (beta_h, last_shift)):
-                nc.sync.dma_start(out=tile[:], in_=vec[H - BANK : H].partition_broadcast(P))
 
             TURN_ROUND = (1, 2, 4, 5, 6)
             LAST_PASS = [TURN_ROUND[-1] + 1] + [(b + 1) * U_PASSES - 1 + QUANTISE_LAG for b in range(1, BLOCKS)]
@@ -424,40 +407,32 @@ def tile_recurrentffn_pb_kernel(
             nc.gpsimd.tensor_tensor(out=off[:], in0=neg_mean[:], in1=neg_centre[:], op=ALU.subtract)
             nc.gpsimd.tensor_tensor(out=off_sq[:], in0=off[:], in1=off[:], op=ALU.mult)
             nc.gpsimd.tensor_tensor(out=var_rest[:], in0=part_var[:], in1=off_sq[:], op=ALU.subtract)
-            pieces = D_PASSES - 1
             gain = [spread(GAMMA_H_AT + g * H_TILES, psum_diff, "diff") for g in range(2)]
-            shift = [spread(BETA_H_AT + g * H_TILES, psum_acc, "acc") for g in range(pieces)]
+            shift = [spread(BETA_H_AT + g * H_TILES, psum_acc, "acc") for g in range(D_PASSES)]
             regroup_chunk(WU_CHUNKS + 1, on_scalar=True)
-            for g in range(pieces):
+            for g in range(D_PASSES):
                 for t in range(B_TILES):
                     apply_gain(t, g, gain[g])
-                if g + 2 < pieces:
+                if g + 2 < D_PASSES:
                     gain.append(spread(GAMMA_H_AT + (g + 2) * H_TILES, psum_diff, "diff"))
-                if g == 0:
+                if g == 1:
                     nc.vector.scalar_tensor_tensor(
                         out=var_eps[:], in0=sq_sums[:, last, :], scalar=1.0 / H, in1=var_rest[:], op0=ALU.mult, op1=ALU.add
                     )
                     nc.gpsimd.tensor_tensor(out=rstd[:], in0=var_eps[:], in1=neg_half[:], op=ALU.pow)
-                    for t in range(B_TILES):
-                        normalise_on_gpsimd(t, pieces)
             regroup_chunk(WU_CHUNKS + 2, on_scalar=True)
             b_d_bank = spread(B_D_AT, psum_turn, "turn")
             nc.scalar.copy(out=b_d_all[:], in_=b_d_bank[:])
             quantise_chunk(WU_CHUNKS)
-            for g in range(pieces):
+            for g in range(D_PASSES):
                 apply_shift(0, g, shift[g])
-                store_and_turn(0, g)
-            store_and_turn(0, pieces)
             regroup_chunk(WU_CHUNKS + 3, on_scalar=True)
             quantise_chunk(WU_CHUNKS + 1)
             apply_shift(1, 0, shift[0])
-            store_and_turn(1, 0)
             quantise_new_h(0, 0, D_PASSES)
             quantise_chunk(WU_CHUNKS + 2)
-            for g in range(1, pieces):
+            for g in range(1, D_PASSES):
                 apply_shift(1, g, shift[g])
-                store_and_turn(1, g)
-            store_and_turn(1, pieces)
             quantise_chunk(WU_CHUNKS + 3)
             second_matmul(0, 0, D_PASSES)
             out_gain = spread(GAMMA_O_AT, psum_acc, "acc")

@@ -281,7 +281,7 @@ def tile_recurrentffn_pb_kernel(
         out_sb = const.tile([P, B_TILES, D], F32, name="out_sb")
         out_stats = [[work.tile([P, 1], F32, name="out_%s%d" % (what, t)) for what in ("sum", "mean", "sq", "rstd")] for t in range(B_TILES)]
 
-        def output_sums(t, gain):
+        def output_sums(t):
             total, neg, sq, rs = out_stats[t]
             nc.vector.scalar_tensor_tensor(
                 out=pre_out[:, t, :], in0=out_acc[t][:], scalar=1.0, in1=b_d_all[:],
@@ -293,16 +293,20 @@ def tile_recurrentffn_pb_kernel(
                 out=squares[:], in_=pre_out[:, t, :], func=ACT.Square, bias=neg[:], scale=1.0, accum_out=sq[:]
             )
             nc.scalar.activation(out=rs[:], in_=sq[:], func=ACT.Abs_reciprocal_sqrt, bias=EPS, scale=1.0 / D)
+
+        def output_gain(t, gain):
             nc.vector.scalar_tensor_tensor(
-                out=out_sb[:, t, :], in0=pre_out[:, t, :], scalar=neg[:], in1=gain[:], op0=ALU.add, op1=ALU.mult
+                out=out_sb[:, t, :], in0=pre_out[:, t, :], scalar=out_stats[t][1][:], in1=gain[:], op0=ALU.add, op1=ALU.mult
             )
 
-        def output_shift(t, shift):
-            nc.vector.scalar_tensor_tensor(
-                out=out_sb[:, t, :], in0=out_sb[:, t, :], scalar=out_stats[t][3][:], in1=shift[:],
-                op0=ALU.mult, op1=ALU.add,
-            )
-            nc.sync.dma_start(out=out_0[t * P : (t + 1) * P, :], in_=out_sb[:, t, :])
+        def output_shift(t, shift, pieces):
+            for piece in range(pieces):
+                cols = slice(piece * D // pieces, (piece + 1) * D // pieces)
+                nc.vector.scalar_tensor_tensor(
+                    out=out_sb[:, t, cols], in0=out_sb[:, t, cols], scalar=out_stats[t][3][:], in1=shift[:, cols],
+                    op0=ALU.mult, op1=ALU.add,
+                )
+                nc.sync.dma_start(out=out_0[t * P : (t + 1) * P, cols], in_=out_sb[:, t, cols])
 
         with tc.manual_schedule():
             by_tile = lambda dram: dram.rearrange("(t r) k -> r t k", r=P)
@@ -379,6 +383,7 @@ def tile_recurrentffn_pb_kernel(
                     if since[b] == 0:
                         turn_difference(b, 1)
                 if i == LAST_PASS[-1] + 4:
+                    quantise_chunk(WU_CHUNKS)
                     part_sum = work.tile([P, B_TILES], F32, name="part_sum")
                     nc.vector.tensor_reduce(
                         out=part_sum[:], in_=blend_sums[:, 0 : BLOCKS - 1].rearrange("p b t -> p t b"), axis=mybir.AxisListType.X, op=ALU.add
@@ -423,25 +428,26 @@ def tile_recurrentffn_pb_kernel(
             regroup_chunk(WU_CHUNKS + 2, on_scalar=True)
             b_d_bank = spread(B_D_AT, psum_turn, "turn")
             nc.scalar.copy(out=b_d_all[:], in_=b_d_bank[:])
-            quantise_chunk(WU_CHUNKS)
             for g in range(D_PASSES):
                 apply_shift(0, g, shift[g])
             regroup_chunk(WU_CHUNKS + 3, on_scalar=True)
             quantise_chunk(WU_CHUNKS + 1)
             apply_shift(1, 0, shift[0])
-            quantise_new_h(0, 0, D_PASSES)
+            out_gain = spread(GAMMA_O_AT, psum_acc, "acc")
             quantise_chunk(WU_CHUNKS + 2)
-            for g in range(1, D_PASSES):
+            apply_shift(1, 1, shift[1])
+            quantise_new_h(0, 0, D_PASSES)
+            for g in range(2, D_PASSES):
                 apply_shift(1, g, shift[g])
             quantise_chunk(WU_CHUNKS + 3)
             second_matmul(0, 0, D_PASSES)
-            out_gain = spread(GAMMA_O_AT, psum_acc, "acc")
+            for first, end in ((0, 2), (2, 3), (3, 4)):
+                quantise_new_h(1, first, end)
+                second_matmul(1, first, end)
             out_shift = spread(BETA_O_AT, psum_acc, "acc")
-            quantise_new_h(1, 0, 2)
-            second_matmul(1, 0, 2)
-            quantise_new_h(1, 2, 4)
-            second_matmul(1, 2, 4)
-            output_sums(0, out_gain)
-            output_sums(1, out_gain)
-            output_shift(0, out_shift)
-            output_shift(1, out_shift)
+            output_sums(0)
+            output_gain(0, out_gain)
+            output_sums(1)
+            output_shift(0, out_shift, pieces=1)
+            output_gain(1, out_gain)
+            output_shift(1, out_shift, pieces=2)

@@ -111,6 +111,13 @@ def tile_recurrentffn_pb_kernel(
             else:
                 nc.vector.tensor_copy(out=dst, in_=src)
 
+        def regroup_on_gpsimd(i):
+            groupeds[i] = grouped_pool.tile([P, BANK, PACK], BF16, name="grouped", tag="grouped", align_bytes=64)
+            nc.gpsimd.tensor_scalar(
+                out=groupeds[i][:].rearrange("q (c i) j -> q c j i", i=RUN), in0=raws[i][:].rearrange("q j (c i) -> q c j i", i=RUN),
+                scalar1=1.0, scalar2=0.0, op0=ALU.mult, op1=ALU.add,
+            )
+
         def quantise_chunk(i):
             if i < WU_CHUNKS:
                 codes, scales = wu_codes[:, i, :], wu_scales[:, i, :]
@@ -332,7 +339,7 @@ def tile_recurrentffn_pb_kernel(
             TURN_ROUND = (1, 2, 4, 5, 6)
             LAST_PASS = [TURN_ROUND[-1] + 1] + [(b + 1) * U_PASSES - 1 + QUANTISE_LAG for b in range(1, BLOCKS)]
 
-            SLACK = [1] * (BLOCKS - 1) + [0]
+            SLACK = [1, 1, 0, 0]
 
             def pass_round(i):
                 block, g = divmod(i, U_PASSES)
@@ -425,12 +432,12 @@ def tile_recurrentffn_pb_kernel(
                         out=var_eps[:], in0=sq_sums[:, last, :], scalar=1.0 / H, in1=var_rest[:], op0=ALU.mult, op1=ALU.add
                     )
                     nc.gpsimd.tensor_tensor(out=rstd[:], in0=var_eps[:], in1=neg_half[:], op=ALU.pow)
+                    regroup_on_gpsimd(WU_CHUNKS + 3)
             regroup_chunk(WU_CHUNKS + 2, on_scalar=True)
             b_d_bank = spread(B_D_AT, psum_turn, "turn")
             nc.scalar.copy(out=b_d_all[:], in_=b_d_bank[:])
             for g in range(D_PASSES):
                 apply_shift(0, g, shift[g])
-            regroup_chunk(WU_CHUNKS + 3, on_scalar=True)
             quantise_chunk(WU_CHUNKS + 1)
             apply_shift(1, 0, shift[0])
             out_gain = spread(GAMMA_O_AT, psum_acc, "acc")

from contextlib import ExitStack

import concourse.mybir as mybir
from concourse.masks import make_identity

F32 = mybir.dt.float32
BF16 = mybir.dt.bfloat16
U32 = mybir.dt.uint32
U8 = mybir.dt.uint8
FP8X4 = mybir.dt.float8_e4m3fn_x4
ALU = mybir.AluOpType
ACT = mybir.ActivationFunctionType

P = 128
PACK = 4
K_PASS = P * PACK
BANK = 512

B, D, H = 256, 512, 2048
C = D + H
EPS = 1e-3
B_TILES = B // P
U_PASSES = C // K_PASS
D_PASSES = H // K_PASS
BLOCKS = H // BANK
H_TILES = BANK // P
PAIRS = H_TILES // 2
WU_CHUNKS = BLOCKS * U_PASSES
CHUNKS = WU_CHUNKS + D_PASSES
BU_COLS = H // P
GAMMA_H_AT, BETA_H_AT = 0, H // P
B_D_AT, GAMMA_O_AT, BETA_O_AT = 2 * H // P, 2 * H // P + D // P, 2 * H // P + 2 * D // P
REST_COLS = 2 * H // P + 3 * D // P

RUN = 8
QUANTISE_LAG = 2

FLOPS = 2 * B * C * H + 2 * B * H * D


def tile_recurrentffn_pb_kernel(
    tc, x, hidden_state, swiglu, W_u, b_u, gamma_h, beta_h, W_d, b_d, gamma_o, beta_o, out_0, out_1
):
    nc = tc.nc
    with ExitStack() as ctx:
        const = ctx.enter_context(tc.tile_pool(name="const", bufs=1))
        raw_pool = ctx.enter_context(tc.tile_pool(name="raw", bufs=8))
        grouped_pool = ctx.enter_context(tc.tile_pool(name="grouped", bufs=4))
        work = ctx.enter_context(tc.tile_pool(name="work", bufs=2))
        psum_acc = ctx.enter_context(tc.psum_pool(name="psum_acc", bufs=4))
        psum_diff = ctx.enter_context(tc.psum_pool(name="psum_diff", bufs=2))
        psum_turn = ctx.enter_context(tc.psum_pool(name="psum_turn", bufs=2))

        ident = const.tile([P, P], F32, name="ident")
        make_identity(nc, ident[:])
        plus_ident = const.tile([P, P], BF16, name="plus_ident")
        make_identity(nc, plus_ident[:])
        minus_ident = const.tile([P, P], BF16, name="minus_ident")
        nc.vector.tensor_scalar_mul(out=minus_ident[:], in0=plus_ident[:], scalar1=-1.0)
        neg_half = const.tile([P, B_TILES], F32, name="neg_half")
        nc.vector.memset(neg_half[:], -0.5)

        warm = const.tile([P, 1], F32, name="warm")
        nc.scalar.activation(out=warm[:], in_=neg_half[:, 0:1], func=ACT.Sigmoid)

        bu_rows = const.tile([P, P], BF16, name="bu_rows")
        nc.vector.memset(bu_rows[:], 0.0)
        bu_cols = const.tile([P, BU_COLS], F32, name="bu_cols")
        rest_rows = const.tile([P, P], BF16, name="rest_rows")
        nc.vector.memset(rest_rows[:], 0.0)
        rest_cols = const.tile([P, REST_COLS], F32, name="rest_cols")
        b_d_all = const.tile([P, D], F32, name="b_d_all")

        def turn_rows(rows):
            turned = psum_turn.tile([P, P], BF16, name="rows_turned", tag="turn")
            nc.tensor.transpose(turned[:], rows[:], plus_ident[:])
            return turned

        def spread(at, pool, tag):
            bank = pool.tile([P, BANK], F32, name="spread_bank", tag=tag)
            for c in range(BANK // P):
                nc.tensor.transpose(
                    bank[:, c * P : (c + 1) * P], rest_cols[:, at + c : at + c + 1].to_broadcast([P, P]), ident[:]
                )
            return bank

        wu_codes = const.tile([P, WU_CHUNKS, BANK], U32, name="wu_codes", align_bytes=64)
        wu_scales = const.tile([P, WU_CHUNKS, BANK], U8, name="wu_scales", align_bytes=64)
        wd_codes = const.tile([P, D_PASSES, D], U32, name="wd_codes", align_bytes=64)
        wd_scales = const.tile([P, D_PASSES, D], U8, name="wd_scales", align_bytes=64)
        raws, groupeds = [], {}

        def load_chunk(i):
            if i < WU_CHUNKS:
                block, g = divmod(i, U_PASSES)
                view = W_u[g * K_PASS : (g + 1) * K_PASS, block * BANK : (block + 1) * BANK].rearrange(
                    "(q j) w -> q j w", j=PACK
                )
            else:
                g = i - WU_CHUNKS
                view = W_d[g * K_PASS : (g + 1) * K_PASS, :].rearrange("(j q) w -> q j w", q=P)
            raws.append(raw_pool.tile([P, PACK, BANK], BF16, name="raw", tag="raw"))
            nc.sync.dma_start(out=raws[i][:], in_=view)

        def regroup_chunk(i, on_scalar):
            groupeds[i] = grouped_pool.tile([P, BANK, PACK], BF16, name="grouped", tag="grouped", align_bytes=64)
            src = raws[i][:].rearrange("q j (c i) -> q c j i", i=RUN)
            dst = groupeds[i][:].rearrange("q (c i) j -> q c j i", i=RUN)
            if on_scalar:
                nc.scalar.copy(out=dst, in_=src)
            else:
                nc.vector.tensor_copy(out=dst, in_=src)

        def regroup_on_gpsimd(i):
            groupeds[i] = grouped_pool.tile([P, BANK, PACK], BF16, name="grouped", tag="grouped", align_bytes=64)
            nc.gpsimd.tensor_scalar(
                out=groupeds[i][:].rearrange("q (c i) j -> q c j i", i=RUN), in0=raws[i][:].rearrange("q j (c i) -> q c j i", i=RUN),
                scalar1=1.0, scalar2=0.0, op0=ALU.mult, op1=ALU.add,
            )

        def quantise_chunk(i):
            if i < WU_CHUNKS:
                codes, scales = wu_codes[:, i, :], wu_scales[:, i, :]
            else:
                codes, scales = wd_codes[:, i - WU_CHUNKS, :], wd_scales[:, i - WU_CHUNKS, :]
            nc.vector.quantize_mx(
                out=codes.bitcast(FP8X4), scales=scales, in_=groupeds[i][:].rearrange("q w j -> q (w j)")
            )

        x_sb = const.tile([P, B_TILES, D], BF16, name="x_sb")
        h_blocks = [const.tile([P, B_TILES, BANK], BF16, name="h_block%d" % b) for b in range(BLOCKS)]
        s_blocks = [const.tile([P, B_TILES, BANK], BF16, name="s_block%d" % b) for b in range(BLOCKS)]
        comb_grouped = const.tile([P, U_PASSES, B, PACK], BF16, name="comb_grouped", align_bytes=64)
        comb_codes = const.tile([P, U_PASSES, B], U32, name="comb_codes", align_bytes=64)
        comb_scales = const.tile([P, U_PASSES, B], U8, name="comb_scales", align_bytes=64)

        def turn_activations(g):
            turned = psum_turn.tile([P, 2, B], F32, name="turned", tag="turn")
            for t in range(B_TILES):
                feats = x_sb[:, t, :] if g == 0 else h_blocks[g - 1][:, t, :]
                words = feats.bitcast(F32).rearrange("r (q u) -> r u q", u=2)
                for u in range(2):
                    nc.tensor.transpose(turned[:, u, t * P : (t + 1) * P], words[:, u, :], ident[:])
            nc.scalar.copy(
                out=comb_grouped[:, g].rearrange("q r j -> q (r j)").bitcast(F32).rearrange("q (r u) -> q r u", u=2),
                in_=turned[:].rearrange("q u r -> q r u"),
            )

        def quantise_activations(g):
            nc.vector.quantize_mx(
                out=comb_codes[:, g, :].bitcast(FP8X4),
                scales=comb_scales[:, g, :],
                in_=comb_grouped[:, g].rearrange("q r j -> q (r j)"),
            )

        blend = const.tile([P, B_TILES, H], F32, name="blend")
        blend_sums = const.tile([P, BLOCKS, B_TILES], F32, name="blend_sums")
        sq_sums = const.tile([P, BLOCKS, B_TILES], F32, name="sq_sums")
        neg_centre = const.tile([P, B_TILES], F32, name="neg_centre")
        accs, diffs, gates, product_banks = {}, {}, {}, {}

        def turn_difference(block, pair):
            diff = psum_diff.tile([P, 2, B], F32, name="diff", tag="diff")
            diffs[block, pair] = diff
            for half in range(2):
                feats = slice((2 * pair + half) * P, (2 * pair + half + 1) * P)
                for t in range(B_TILES):
                    rows = slice(t * P, (t + 1) * P)
                    nc.tensor.matmul(
                        out=diff[:, half, rows], lhsT=s_blocks[block][:, t, feats], rhs=plus_ident[:], start=True, stop=False
                    )
                    nc.tensor.matmul(
                        out=diff[:, half, rows], lhsT=h_blocks[block][:, t, feats], rhs=minus_ident[:], start=False, stop=True
                    )

        def first_matmul(i):
            block, g = divmod(i, U_PASSES)
            for c in range(H_TILES):
                if g == 0:
                    accs[block, c] = psum_acc.tile([P, BANK], F32, name="acc", tag="acc")
                m_cols = slice(c * P, (c + 1) * P)
                nc.tensor.matmul_mx(
                    out=accs[block, c][:, 0:B],
                    lhsT=wu_codes[:, i, m_cols].bitcast(FP8X4),
                    lhsT_scale=wu_scales[:, i, m_cols],
                    rhs=comb_codes[:, g, :].bitcast(FP8X4),
                    rhs_scale=comb_scales[:, g, :],
                    start=(g == 0),
                    stop=(g == U_PASSES - 1),
                )

        def sigmoid(block, pair):
            gate = work.tile([P, 2, B], F32, name="gate", tag="gate")
            gates[block, pair] = gate
            for half in range(2):
                c = 2 * pair + half
                tile = block * H_TILES + c
                nc.scalar.activation(
                    out=gate[:, half, :], in_=accs[block, c][:, 0:B], func=ACT.Sigmoid,
                    bias=bu_cols[:, tile : tile + 1], scale=1.0,
                )

        def gate_difference(block, pair):
            gate = gates[block, pair]
            nc.vector.tensor_tensor(out=gate[:], in0=gate[:], in1=diffs[block, pair][:], op=ALU.mult)

        def turn_product(block, pair):
            for t in range(B_TILES):
                if pair == 0:
                    product_banks[block, t] = psum_turn.tile([P, BANK], F32, name="product_bank", tag="turn")
                for half in range(2):
                    c = 2 * pair + half
                    nc.tensor.transpose(
                        product_banks[block, t][:, c * P : (c + 1) * P], gates[block, pair][:, half, t * P : (t + 1) * P], ident[:]
                    )

        def add_hidden(block):
            cols = slice(block * BANK, (block + 1) * BANK)
            for t in range(B_TILES):
                nc.vector.scalar_tensor_tensor(
                    out=blend[:, t, cols], in0=h_blocks[block][:, t, :], scalar=2.0, in1=product_banks[block, t][:],
                    op0=ALU.mult, op1=ALU.add, accum_out=blend_sums[:, block, t : t + 1],
                )
            if block == 0:
                nc.vector.tensor_scalar_mul(out=neg_centre[:], in0=blend_sums[:, 0, :], scalar1=-1.0 / BANK)

        def square_sums(block):
            cols = slice(block * BANK, (block + 1) * BANK)
            for t in range(B_TILES):
                squares = work.tile([P, BANK], BF16, name="squares", tag="squares")
                nc.scalar.activation(
                    out=squares[:], in_=blend[:, t, cols], func=ACT.Square,
                    bias=neg_centre[:, t : t + 1], scale=1.0, accum_out=sq_sums[:, block, t : t + 1],
                )

        new_h = const.tile([P, B_TILES, H], F32, name="new_h")
        nh_grouped = const.tile([P, B_TILES, D_PASSES, P, PACK], BF16, name="nh_grouped", align_bytes=64)
        nh_codes = const.tile([P, B_TILES, D_PASSES, P], U32, name="nh_codes", align_bytes=64)
        nh_scales = const.tile([P, B_TILES, D_PASSES, P], U8, name="nh_scales", align_bytes=64)
        neg_mean = const.tile([P, B_TILES], F32, name="neg_mean")
        rstd = const.tile([P, B_TILES], F32, name="rstd")

        def apply_gain(t, g, gain):
            cols = slice(g * K_PASS, (g + 1) * K_PASS)
            nc.vector.scalar_tensor_tensor(
                out=new_h[:, t, cols], in0=blend[:, t, cols], scalar=neg_mean[:, t : t + 1], in1=gain[:],
                op0=ALU.add, op1=ALU.mult,
            )

        def apply_shift(t, g, shift):
            cols = slice(g * K_PASS, (g + 1) * K_PASS)
            nc.vector.scalar_tensor_tensor(
                out=new_h[:, t, cols], in0=new_h[:, t, cols], scalar=rstd[:, t : t + 1], in1=shift[:],
                op0=ALU.mult, op1=ALU.add,
            )
            nc.sync.dma_start(out=out_1[t * P : (t + 1) * P, cols], in_=new_h[:, t, cols])
            pool, tag = (psum_turn, "turn") if g % 2 == 0 else (psum_diff, "diff")
            turned = pool.tile([P, PACK, P], F32, name="nh_turned", tag=tag)
            for j in range(PACK):
                k0 = g * K_PASS + j * P
                nc.tensor.transpose(turned[:, j, :], new_h[:, t, k0 : k0 + P], ident[:])
            nc.scalar.copy(out=nh_grouped[:, t, g], in_=turned[:].rearrange("q j r -> q r j"))

        def quantise_new_h(t, first, last):
            nc.vector.quantize_mx(
                out=nh_codes[:, t, first:last].rearrange("q g r -> q (g r)").bitcast(FP8X4),
                scales=nh_scales[:, t, first:last].rearrange("q g r -> q (g r)"),
                in_=nh_grouped[:, t, first:last].rearrange("q g r j -> q (g r j)"),
            )

        out_acc = {}

        def second_matmul(t, first, last):
            if first == 0:
                out_acc[t] = psum_acc.tile([P, D], F32, name="out_acc", tag="acc")
            for g in range(first, last):
                nc.tensor.matmul_mx(
                    out=out_acc[t][:],
                    lhsT=nh_codes[:, t, g, :].bitcast(FP8X4),
                    lhsT_scale=nh_scales[:, t, g, :],
                    rhs=wd_codes[:, g, :].bitcast(FP8X4),
                    rhs_scale=wd_scales[:, g, :],
                    start=(g == 0),
                    stop=(g == D_PASSES - 1),
                )

        pre_out = const.tile([P, B_TILES, D], F32, name="pre_out")
        out_sb = const.tile([P, B_TILES, D], F32, name="out_sb")
        out_stats = [[work.tile([P, 1], F32, name="out_%s%d" % (what, t)) for what in ("sum", "mean", "sq", "rstd")] for t in range(B_TILES)]

        def output_sums(t):
            total, neg, sq, rs = out_stats[t]
            nc.vector.scalar_tensor_tensor(
                out=pre_out[:, t, :], in0=out_acc[t][:], scalar=1.0, in1=b_d_all[:],
                op0=ALU.mult, op1=ALU.add, accum_out=total[:],
            )
            nc.vector.tensor_scalar_mul(out=neg[:], in0=total[:], scalar1=-1.0 / D)
            squares = work.tile([P, BANK], BF16, name="squares", tag="squares")
            nc.scalar.activation(
                out=squares[:], in_=pre_out[:, t, :], func=ACT.Square, bias=neg[:], scale=1.0, accum_out=sq[:]
            )
            nc.scalar.activation(out=rs[:], in_=sq[:], func=ACT.Abs_reciprocal_sqrt, bias=EPS, scale=1.0 / D)

        def output_gain(t, gain):
            nc.vector.scalar_tensor_tensor(
                out=out_sb[:, t, :], in0=pre_out[:, t, :], scalar=out_stats[t][1][:], in1=gain[:], op0=ALU.add, op1=ALU.mult
            )

        def output_shift(t, shift, pieces):
            for piece in range(pieces):
                cols = slice(piece * D // pieces, (piece + 1) * D // pieces)
                nc.vector.scalar_tensor_tensor(
                    out=out_sb[:, t, cols], in0=out_sb[:, t, cols], scalar=out_stats[t][3][:], in1=shift[:, cols],
                    op0=ALU.mult, op1=ALU.add,
                )
                nc.sync.dma_start(out=out_0[t * P : (t + 1) * P, cols], in_=out_sb[:, t, cols])

        with tc.manual_schedule():
            by_tile = lambda dram: dram.rearrange("(t r) k -> r t k", r=P)
            rest_vectors = ((gamma_h, GAMMA_H_AT), (beta_h, BETA_H_AT), (b_d, B_D_AT), (gamma_o, GAMMA_O_AT), (beta_o, BETA_O_AT))
            H_LOADED_BEHIND = (1, 3, 4, 5)
            for i in range(CHUNKS):
                load_chunk(i)
                if i == 1:
                    nc.sync.dma_start(out=x_sb[:], in_=by_tile(x))
                if i in H_LOADED_BEHIND:
                    b = H_LOADED_BEHIND.index(i)
                    cols = slice(b * BANK, (b + 1) * BANK)
                    nc.sync.dma_start(out=h_blocks[b][:], in_=by_tile(hidden_state)[:, :, cols])
                if 2 < i <= 2 + len(rest_vectors):
                    vec, at = rest_vectors[i - 3]
                    nc.sync.dma_start(out=rest_rows[at : at + vec.shape[0] // P, :], in_=vec.rearrange("(c q) -> c q", q=P))
                if i == 2:
                    nc.sync.dma_start(out=bu_rows[0:BU_COLS, :], in_=b_u.rearrange("(c q) -> c q", q=P))
                if i < WU_CHUNKS and i % U_PASSES == U_PASSES - 1:
                    cols = slice(i // U_PASSES * BANK, (i // U_PASSES + 1) * BANK)
                    nc.sync.dma_start(out=s_blocks[i // U_PASSES][:], in_=by_tile(swiglu)[:, :, cols])

            TURN_ROUND = (1, 2, 4, 5, 6)
            LAST_PASS = [TURN_ROUND[-1] + 1] + [(b + 1) * U_PASSES - 1 + QUANTISE_LAG for b in range(1, BLOCKS)]

            SLACK = [1, 1, 0, 0]

            def pass_round(i):
                block, g = divmod(i, U_PASSES)
                if block == 0:
                    return TURN_ROUND[g] + 1
                return max(i + QUANTISE_LAG, LAST_PASS[block - 1] + SLACK[block - 1] + 2)

            for i in range(LAST_PASS[-1] + 6):
                since = [i - last - slack for last, slack in zip(LAST_PASS, SLACK)]
                for b in range(BLOCKS):
                    if since[b] in (1, 2):
                        sigmoid(b, since[b] - 1)
                    if since[b] in (3, 4):
                        turn_product(b, since[b] - 3)
                    if since[b] == -1:
                        turn_difference(b, 0)
                for b in range(BLOCKS - 1):
                    if since[b] == 7:
                        square_sums(b)
                if i < WU_CHUNKS:
                    regroup_chunk(i, on_scalar=(i % U_PASSES in (1, 3)))
                if i == WU_CHUNKS:
                    regroup_chunk(WU_CHUNKS, on_scalar=True)
                if 0 <= i - QUANTISE_LAG < WU_CHUNKS:
                    quantise_chunk(i - QUANTISE_LAG)
                for g in range(U_PASSES):
                    if i == TURN_ROUND[g]:
                        turn_activations(g)
                    if i == TURN_ROUND[g] + 1:
                        quantise_activations(g)
                if i == U_PASSES:
                    bu_turned = turn_rows(bu_rows)
                if i == U_PASSES + 1:
                    nc.vector.tensor_copy(out=bu_cols[:], in_=bu_turned[:, 0:BU_COLS])
                if i == TURN_ROUND[-1] + 1:
                    rest_turned = turn_rows(rest_rows)
                if i == TURN_ROUND[-1] + 2:
                    nc.vector.tensor_copy(out=rest_cols[:], in_=rest_turned[:, 0:REST_COLS])
                for b in range(BLOCKS):
                    if since[b] == 5:
                        add_hidden(b)
                    if since[b] in (2, 3):
                        gate_difference(b, since[b] - 2)
                for chunk in range(WU_CHUNKS):
                    if i == pass_round(chunk):
                        first_matmul(chunk)
                for b in range(BLOCKS):
                    if since[b] == 0:
                        turn_difference(b, 1)
                if i == LAST_PASS[-1] + 4:
                    quantise_chunk(WU_CHUNKS)
                    part_sum = work.tile([P, B_TILES], F32, name="part_sum")
                    nc.vector.tensor_reduce(
                        out=part_sum[:], in_=blend_sums[:, 0 : BLOCKS - 1].rearrange("p b t -> p t b"), axis=mybir.AxisListType.X, op=ALU.add
                    )
                    part_neg_mean = work.tile([P, B_TILES], F32, name="part_neg_mean")
                    nc.vector.tensor_scalar_mul(out=part_neg_mean[:], in0=part_sum[:], scalar1=-1.0 / H)

            last = BLOCKS - 1
            nc.scalar.activation(out=warm[:], in_=neg_half[:, 0:1], func=ACT.Abs_reciprocal_sqrt)
            square_sums(last)
            nc.vector.scalar_tensor_tensor(
                out=neg_mean[:], in0=blend_sums[:, last, :], scalar=-1.0 / H, in1=part_neg_mean[:], op0=ALU.mult, op1=ALU.add
            )
            part_sq = work.tile([P, B_TILES], F32, name="part_sq")
            nc.vector.tensor_reduce(
                out=part_sq[:], in_=sq_sums[:, 0:last].rearrange("p b t -> p t b"), axis=mybir.AxisListType.X, op=ALU.add
            )
            part_var = work.tile([P, B_TILES], F32, name="part_var")
            nc.gpsimd.tensor_scalar(
                out=part_var[:], in0=part_sq[:], scalar1=1.0 / H, scalar2=EPS, op0=ALU.mult, op1=ALU.add
            )
            off = work.tile([P, B_TILES], F32, name="off")
            off_sq = work.tile([P, B_TILES], F32, name="off_sq")
            var_rest = work.tile([P, B_TILES], F32, name="var_rest")
            var_eps = work.tile([P, B_TILES], F32, name="var_eps")
            nc.gpsimd.tensor_tensor(out=off[:], in0=neg_mean[:], in1=neg_centre[:], op=ALU.subtract)
            nc.gpsimd.tensor_tensor(out=off_sq[:], in0=off[:], in1=off[:], op=ALU.mult)
            nc.gpsimd.tensor_tensor(out=var_rest[:], in0=part_var[:], in1=off_sq[:], op=ALU.subtract)
            gain = [spread(GAMMA_H_AT + g * H_TILES, psum_diff, "diff") for g in range(2)]
            shift = [spread(BETA_H_AT + g * H_TILES, psum_acc, "acc") for g in range(D_PASSES)]
            regroup_chunk(WU_CHUNKS + 1, on_scalar=True)
            for g in range(D_PASSES):
                for t in range(B_TILES):
                    apply_gain(t, g, gain[g])
                if g + 2 < D_PASSES:
                    gain.append(spread(GAMMA_H_AT + (g + 2) * H_TILES, psum_diff, "diff"))
                if g == 1:
                    nc.vector.scalar_tensor_tensor(
                        out=var_eps[:], in0=sq_sums[:, last, :], scalar=1.0 / H, in1=var_rest[:], op0=ALU.mult, op1=ALU.add
                    )
                    nc.gpsimd.tensor_tensor(out=rstd[:], in0=var_eps[:], in1=neg_half[:], op=ALU.pow)
                    regroup_on_gpsimd(WU_CHUNKS + 3)
            regroup_chunk(WU_CHUNKS + 2, on_scalar=True)
            b_d_bank = spread(B_D_AT, psum_turn, "turn")
            nc.scalar.copy(out=b_d_all[:], in_=b_d_bank[:])
            for g in range(D_PASSES):
                apply_shift(0, g, shift[g])
            quantise_chunk(WU_CHUNKS + 1)
            apply_shift(1, 0, shift[0])
            out_gain = spread(GAMMA_O_AT, psum_acc, "acc")
            quantise_chunk(WU_CHUNKS + 2)
            apply_shift(1, 1, shift[1])
            quantise_new_h(0, 0, D_PASSES)
            for g in range(2, D_PASSES):
                apply_shift(1, g, shift[g])
            quantise_chunk(WU_CHUNKS + 3)
            second_matmul(0, 0, D_PASSES)
            for first, end in ((0, 2), (2, 3), (3, 4)):
                quantise_new_h(1, first, end)
                second_matmul(1, first, end)
            out_shift = spread(BETA_O_AT, psum_acc, "acc")
            output_sums(0)
            output_gain(0, out_gain)
            output_sums(1)
            output_shift(0, out_shift, pieces=1)
            output_gain(1, out_gain)
            output_shift(1, out_shift, pieces=2)
